import numpy as np
import ml_dtypes


def mxq(x, axis, fmt="e4m3"):
    dtype, down = {"e4m3": (ml_dtypes.float8_e4m3fn, 7), "e5m2": (ml_dtypes.float8_e5m2, 14)}[fmt]
    v = np.moveaxis(np.asarray(x, np.float32).astype(ml_dtypes.bfloat16).astype(np.float64), axis, -1)
    blocks = v.reshape(v.shape[:-1] + (-1, 32))
    amax = np.abs(blocks).max(-1, keepdims=True)
    byte = np.maximum(np.where(amax > 0, np.frexp(amax)[1] - 1 + 127, 0) - down, 1)
    scale = np.exp2(byte - 127.0)
    codes = (blocks / scale).astype(np.float32).astype(dtype).astype(np.float64)
    return np.moveaxis((codes * scale).reshape(v.shape), -1, axis)


WIDE = False


def mx_kscale(k):
    if not WIDE:
        return np.ones(k)
    levels = np.array([30, -30])
    if k % 512:
        return np.exp2(np.random.permutation(np.resize(levels, k // 32))).repeat(32)
    a = np.empty((k // 512, 16))
    for p in range(k // 512):
        a[p, :8] = np.random.permutation(np.resize(levels, 8))
        for g in range(8):
            far = levels[np.abs(levels - a[p, g]) >= 10]
            a[p, g + 8] = far[np.random.randint(len(far))]
    return np.exp2(a.ravel()).repeat(32)


BF16 = ml_dtypes.bfloat16


def bf(x):
    return np.asarray(x, np.float32).astype(BF16)


def f64(x):
    return np.asarray(x).astype(np.float64)


S, H, NH, KVH, HD, WIN = 512, 2048, 32, 8, 64, 128
HALF = HD // 2
Q_END = NH * HD
K_END = Q_END + KVH * HD
QKV = K_END + KVH * HD
ROPE_BASE = 10000.0


def rope_rotate(u, cos, sin):
    u1, u2 = u[..., :HALF], u[..., HALF:]
    c, sn = cos[:, None, :], sin[:, None, :]
    return np.concatenate([u1 * c - u2 * sn, u2 * c + u1 * sn], axis=-1)


def setup_inputs():
    s = mx_kscale(H)
    ang = np.arange(S)[:, None] * (1.0 / ROPE_BASE ** (np.arange(HALF) / HALF))[None, :]
    return {"x": bf(np.random.standard_normal((S, H)) * s),
            "qkv_kernel": bf(np.random.standard_normal((H, QKV)) * 1.2 / np.sqrt(H) / s[:, None]),
            "qkv_bias": bf(np.random.standard_normal(QKV) * 0.3),
            "cos_table": bf(np.cos(ang)),
            "sin_table": bf(np.sin(ang))}


def reference(x, qkv_kernel, qkv_bias, cos_table, sin_table):
    qkv = (mxq(f64(x), 1, "e5m2") @ mxq(f64(qkv_kernel), 0, "e5m2")) + f64(qkv_bias)
    cos, sin = f64(cos_table), f64(sin_table)
    q = rope_rotate(qkv[:, :Q_END].reshape(S, NH, HD), cos, sin)
    k = rope_rotate(qkv[:, Q_END:K_END].reshape(S, KVH, HD), cos, sin)
    v = qkv[:, K_END:].reshape(S, KVH, HD)
    return q, k, v

@@ -1,0 +1,267 @@
+from contextlib import ExitStack
+
+import concourse.mybir as mybir
+from concourse.masks import make_identity
+
+S_TOK, H, QKV = 512, 2048, 3072
+FLOPS = 2 * S_TOK * H * QKV
+
+F32 = mybir.dt.float32
+BF16 = mybir.dt.bfloat16
+U32 = mybir.dt.uint32
+U8 = mybir.dt.uint8
+E5X4 = mybir.dt.float8_e5m2_x4
+ADD = mybir.AluOpType.add
+MULT = mybir.AluOpType.mult
+
+P = 128
+NG = 4
+NGRP = 6
+GW = 512
+
+ASG = (("S", "V", "S", "V"), ("S", "S", "G", "V"), ("S", "G", "S", "G"), ("S", "G", "S", "G"), ("S", "G", "S", "G"), ("S", "G", "S", "G"))
+PAT_B = True
+LOOKAHEAD = 4
+
+
+def tile_attentioncore_pa_kernel(tc, x, qkv_kernel, qkv_bias, cos_table, sin_table,
+                                             out_0, out_1, out_2):
+    nc = tc.nc
+    with ExitStack() as ctx:
+        const = ctx.enter_context(tc.tile_pool(name="const", bufs=1))
+        rawp = ctx.enter_context(tc.tile_pool(name="rawp", bufs=2))
+        grpp = ctx.enter_context(tc.tile_pool(name="grpp", bufs=6))
+        codes = ctx.enter_context(tc.tile_pool(name="codes", bufs=1))
+        tup = ctx.enter_context(tc.tile_pool(name="tup", bufs=4))
+        outp = ctx.enter_context(tc.tile_pool(name="outp", bufs=3))
+        accp = ctx.enter_context(tc.psum_pool(name="accp", bufs=4))
+        trp = ctx.enter_context(tc.psum_pool(name="trp", bufs=4))
+        ctx.enter_context(tc.manual_schedule(engines={mybir.EngineType.PE}))
+
+        cos_sb = const.tile([P, 4, 32], BF16, name="cos_sb", tag="cos_sb")
+        sin_sb = const.tile([P, 4, 32], BF16, name="sin_sb", tag="sin_sb")
+        b2d = const.tile([P, P], BF16, name="b2d", tag="b2d")
+        nc.vector.memset(b2d[:], 0.0)
+        nc.scalar.dma_start(out=cos_sb[:], in_=cos_table.rearrange("(i p) j -> p i j", p=P))
+        nc.scalar.dma_start(out=sin_sb[:], in_=sin_table.rearrange("(i p) j -> p i j", p=P))
+        nc.scalar.dma_start(out=b2d[0:24, :], in_=qkv_bias.rearrange("(r c) -> r c", c=P))
+
+        x_sb = const.tile([P, 4, H], BF16, name="x_sb", tag="x_sb")
+        for i in range(4):
+            nc.sync.dma_start(out=x_sb[:, i, :], in_=x[i * P:(i + 1) * P, :])
+        raw01 = rawp.tile([P, 2, NG, 4, GW], BF16, name="raw01", tag="raw")
+        for n in range(2):
+            for g in range(NG):
+                nc.sync.dma_start(
+                    out=raw01[:, n, g, :, :],
+                    in_=qkv_kernel[g * 512:(g + 1) * 512, n * GW:(n + 1) * GW].rearrange(
+                        "(p j) w -> p j w", j=4))
+        raw_wide = []
+        for h in range(2):
+            rw = rawp.tile([P, NG, 4, 2 * GW], BF16, name="raww%d" % h, tag="raw")
+            for g in range(NG):
+                nc.sync.dma_start(
+                    out=rw[:, g, :, :],
+                    in_=qkv_kernel[g * 512:(g + 1) * 512,
+                                   (2 + 2 * h) * GW:(4 + 2 * h) * GW].rearrange(
+                        "(p j) w -> p j w", j=4))
+            raw_wide.append(rw)
+
+        def raw_unit(n, g):
+            if n < 2:
+                return raw01[:, n, g, :, :]
+            return raw_wide[(n - 2) // 2][:, g, :, (n % 2) * GW:(n % 2 + 1) * GW]
+
+        ident_f = const.tile([P, P], F32, name="ident_f", tag="ident_f")
+        make_identity(nc, ident_f[:])
+        ident_b = const.tile([P, P], BF16, name="ident_b", tag="ident_b")
+        nc.vector.tensor_copy(out=ident_b[:], in_=ident_f[:])
+        perm_f = const.tile([P, P], F32, name="perm_f", tag="perm_f")
+        pv = perm_f[:].rearrange("p (a h j) -> p a h j", a=2, h=2)
+        iv = ident_f[:].rearrange("p (a h j) -> p a h j", a=2, h=2)
+        nc.vector.tensor_copy(out=pv[:, :, 0, :], in_=iv[:, :, 1, :])
+        nc.vector.tensor_copy(out=pv[:, :, 1, :], in_=iv[:, :, 0, :])
+
+        e_c = const.tile([P, 4, P], BF16, name="e_c", tag="e_c")
+        e_s = const.tile([P, 4, P], BF16, name="e_s", tag="e_s")
+        for r in range(4):
+            nc.vector.tensor_copy(out=e_c[:, :, r * 32:(r + 1) * 32], in_=cos_sb[:])
+            if r % 2 == 0:
+                nc.vector.tensor_copy(out=e_s[:, :, r * 32:(r + 1) * 32], in_=sin_sb[:])
+            else:
+                nc.vector.tensor_scalar_mul(out=e_s[:, :, r * 32:(r + 1) * 32], in0=sin_sb[:],
+                                            scalar1=-1.0)
+        ct = const.tile([P, S_TOK], BF16, name="ct", tag="ct")
+        snt = const.tile([P, S_TOK], BF16, name="snt", tag="snt")
+        for (src, dst, nm) in ((e_c, ct, "ctp"), (e_s, snt, "sntp")):
+            tb = accp.tile([P, S_TOK], BF16, name=nm, tag="acc")
+            for i in range(4):
+                nc.tensor.transpose(tb[:, i * P:(i + 1) * P], src[:, i, :], ident_b[:])
+            nc.vector.tensor_copy(out=dst[:], in_=tb[:])
+        b_pp = const.tile([P, P], F32, name="b_pp", tag="b_pp")
+        btp = accp.tile([P, P], BF16, name="btp", tag="acc")
+        nc.tensor.transpose(btp[:], b2d[:], ident_b[:])
+        nc.vector.tensor_copy(out=b_pp[:], in_=btp[:])
+        bv_bc = const.tile([P, GW], F32, name="bv_bc", tag="bv_bc")
+        bvp = accp.tile([P, GW], F32, name="bvp", tag="acc")
+        for r in range(4):
+            nc.tensor.matmul(out=bvp[:, r * P:(r + 1) * P],
+                             lhsT=ident_b[:, 20 + r:21 + r].to_broadcast([P, P]),
+                             rhs=b2d[:], start=True, stop=True)
+        nc.vector.tensor_copy(out=bv_bc[:], in_=bvp[:])
+
+        xc = codes.tile([P, NG, S_TOK], U32, name="xc", tag="xc", align_bytes=64)
+        xs = codes.tile([P, NG, S_TOK], U8, name="xs", tag="xs", align_bytes=64)
+        gxs = []
+        for g in range(NG):
+            gx = grpp.tile([P, 4 * S_TOK], BF16, name="gx%d" % g, tag="grp", align_bytes=64)
+            gxs.append(gx)
+        for ip in range(2):
+            for g in range(NG):
+                xt = trp.tile([P, 2, 2, P], F32, name="xt%d%d" % (ip, g), tag="tr")
+                for a in range(2):
+                    words = x_sb[:, 2 * ip + a, :].bitcast(F32)
+                    for u in range(2):
+                        nc.tensor.transpose(xt[:, a, u, :],
+                                            words[:, 256 * g + u:256 * (g + 1):2], ident_f[:])
+                dst = gxs[g][:].bitcast(F32).rearrange("p (i r u) -> p i r u", i=4, u=2)
+                src = xt[:].rearrange("p a u r -> p a r u")
+                if g % 2 == 0:
+                    nc.scalar.copy(out=dst[:, 2 * ip:2 * ip + 2, :, :], in_=src)
+                else:
+                    nc.vector.tensor_copy(out=dst[:, 2 * ip:2 * ip + 2, :, :], in_=src)
+
+        def quant_x(g):
+            nc.vector.quantize_mx(out=xc[:, g, :].bitcast(E5X4), scales=xs[:, g, :], in_=gxs[g][:])
+
+        wcs = []
+        wss = []
+        for n in range(NGRP):
+            wc = codes.tile([P, NG, GW], U32, name="wc%d" % n, tag="wc%d" % n, align_bytes=64)
+            ws = codes.tile([P, NG, GW], U8, name="ws%d" % n, tag="ws%d" % n, align_bytes=64)
+            wcs.append(wc)
+            wss.append(ws)
+        grs = {}
+
+        def copy_unit(n, g):
+            gr = grpp.tile([P, 4 * GW], BF16, name="gr%d%d" % (n, g), tag="grp", align_bytes=64)
+            grs[(n, g)] = gr
+            if PAT_B and ASG[n][g] != "G":
+                dst = gr[:].rearrange("p (c i j) -> p c j i", i=4, j=4)
+                src = raw_unit(n, g).rearrange("p j (c i) -> p c j i", i=4)
+            else:
+                dst = gr[:].rearrange("p (w j) -> p w j", j=4)
+                src = raw_unit(n, g).rearrange("p j w -> p w j")
+            eng = ASG[n][g]
+            if eng == "V":
+                nc.vector.tensor_copy(out=dst, in_=src)
+            elif eng == "S":
+                nc.scalar.copy(out=dst, in_=src)
+            else:
+                nc.gpsimd.tensor_scalar(out=dst, in0=src, scalar1=1.0, scalar2=0.0, op0=MULT, op1=ADD)
+
+        def quant_unit(n, g):
+            nc.vector.quantize_mx(out=wcs[n][:, g, :].bitcast(E5X4), scales=wss[n][:, g, :],
+                                  in_=grs[(n, g)][:])
+
+        q3 = out_0.rearrange("s h d -> s (h d)").rearrange("(i p) c -> p i c", p=P)
+        k3 = out_1.rearrange("s h d -> s (h d)").rearrange("(i p) c -> p i c", p=P)
+        v2 = out_2.rearrange("s h d -> s (h d)")
+
+        accs = {}
+        tus = {}
+        trs = {}
+        outs = {}
+
+        def mx(m, g):
+            if g == 0:
+                acc_new = accp.tile([P, S_TOK], F32, name="acc%d" % m, tag="acc")
+                accs[m] = acc_new
+            if m < 20:
+                n = m // 4
+                cols = slice((m % 4) * P, (m % 4 + 1) * P)
+                nc.tensor.matmul_mx(out=accs[m][:],
+                                    lhsT=wcs[n][:, g, cols].bitcast(E5X4), lhsT_scale=wss[n][:, g, cols],
+                                    rhs=xc[:, g, :].bitcast(E5X4), rhs_scale=xs[:, g, :],
+                                    start=(g == 0), stop=(g == NG - 1))
+            else:
+                cols = slice((m - 20) * P, (m - 19) * P)
+                nc.tensor.matmul_mx(out=accs[m][:],
+                                    lhsT=xc[:, g, cols].bitcast(E5X4), lhsT_scale=xs[:, g, cols],
+                                    rhs=wcs[5][:, g, :].bitcast(E5X4), rhs_scale=wss[5][:, g, :],
+                                    start=(g == 0), stop=(g == NG - 1))
+
+        def rot(m):
+            t_t = tup.tile([P, S_TOK], F32, name="t%d" % m, tag="t")
+            u_t = tup.tile([P, S_TOK], F32, name="u%d" % m, tag="u")
+            tus[m] = (t_t, u_t)
+            nc.vector.scalar_tensor_tensor(out=t_t[:], in0=accs[m][:], scalar=b_pp[:, m:m + 1],
+                                           in1=ct[:], op0=ADD, op1=MULT)
+            nc.vector.scalar_tensor_tensor(out=u_t[:], in0=accs[m][:], scalar=b_pp[:, m:m + 1],
+                                           in1=snt[:], op0=ADD, op1=MULT)
+
+        def back(m):
+            tr = trp.tile([P, 4, P], F32, name="tr%d" % m, tag="tr")
+            trs[m] = tr
+            (t_t, u_t) = tus[m]
+            for i in range(4):
+                nc.tensor.matmul(out=tr[:, i, :], lhsT=t_t[:, i * P:(i + 1) * P], rhs=ident_f[:],
+                                 is_transpose=True, start=True, stop=False)
+                nc.tensor.matmul(out=tr[:, i, :], lhsT=u_t[:, i * P:(i + 1) * P], rhs=perm_f[:],
+                                 is_transpose=True, start=False, stop=True)
+
+        def leave(m):
+            n = m // 4
+            if m % 4 == 0:
+                o_new = outp.tile([P, 4, GW], F32, name="o%d" % n, tag="o")
+                outs[n] = o_new
+            nc.scalar.copy(out=outs[n][:, :, (m % 4) * P:(m % 4 + 1) * P], in_=trs[m][:])
+            if m % 4 == 3:
+                if n < 4:
+                    nc.scalar.dma_start(out=q3[:, :, n * GW:(n + 1) * GW], in_=outs[n][:])
+                else:
+                    nc.scalar.dma_start(out=k3, in_=outs[n][:])
+
+        def v_out(i):
+            vo = outp.tile([P, GW], F32, name="vo%d" % i, tag="vo")
+            nc.vector.tensor_tensor(out=vo[:], in0=accs[20 + i][:], in1=bv_bc[:], op=ADD)
+            nc.sync.dma_start(out=v2[i * P:(i + 1) * P, :], in_=vo[:])
+
+        for g in range(NG):
+            copy_unit(0, g)
+            quant_x(g)
+            quant_unit(0, g)
+            for m in range(4):
+                mx(m, g)
+        units = [(n, g) for n in range(1, NGRP) for g in range(NG)]
+        todo_c = list(units)
+        todo_q = list(units)
+
+        def copies(cnt):
+            for (n, g) in todo_c[:cnt]:
+                copy_unit(n, g)
+            todo_c[:cnt] = []
+
+        def quants(cnt):
+            for (n, g) in todo_q[:cnt]:
+                quant_unit(n, g)
+            todo_q[:cnt] = []
+
+        copies(LOOKAHEAD)
+        for k in range(12):
+            if 1 <= k <= 10:
+                for m in (2 * k + 2, 2 * k + 3):
+                    for g in range(NG):
+                        mx(m, g)
+            for m in (2 * k, 2 * k + 1):
+                if k < 10:
+                    rot(m)
+                else:
+                    v_out(m - 20)
+            if k < 10:
+                back(2 * k)
+                back(2 * k + 1)
+                leave(2 * k)
+                leave(2 * k + 1)
+            quants(4 if k == 0 else 2)
+            copies(2)

@@ -19,7 +19,7 @@ NG = 4
 NGRP = 6
 GW = 512
 
-ASG = (("S", "V", "S", "V"), ("S", "S", "G", "V"), ("S", "G", "S", "G"), ("S", "G", "S", "G"), ("S", "G", "S", "G"), ("S", "G", "S", "G"))
+ASG = (("S", "V", "S", "V"), ("S", "S", "S", "V"), ("S", "V", "S", "S"), ("S", "V", "S", "S"), ("S", "V", "S", "V"), ("S", "V", "S", "V"))
 PAT_B = True
 LOOKAHEAD = 4
 
@@ -146,7 +146,7 @@ def tile_attentioncore_pa_kernel(tc, x, qkv_kernel, qkv_bias, cos_table, sin_tab
         def copy_unit(n, g):
             gr = grpp.tile([P, 4 * GW], BF16, name="gr%d%d" % (n, g), tag="grp", align_bytes=64)
             grs[(n, g)] = gr
-            if PAT_B and ASG[n][g] != "G":
+            if PAT_B:
                 dst = gr[:].rearrange("p (c i j) -> p c j i", i=4, j=4)
                 src = raw_unit(n, g).rearrange("p j (c i) -> p c j i", i=4)
             else:

@@ -18,10 +18,8 @@ P = 128
 NG = 4
 NGRP = 6
 GW = 512
-
-ASG = (("S", "V", "S", "V"), ("S", "S", "S", "V"), ("S", "V", "S", "S"), ("S", "V", "S", "S"), ("S", "V", "S", "V"), ("S", "V", "S", "V"))
+G_UNITS = ((0, 1), (1, 3), (1, 3), (1, 3), (1, 3), (1, 3))
 PAT_B = True
-LOOKAHEAD = 4
 
 
 def tile_attentioncore_pa_kernel(tc, x, qkv_kernel, qkv_bias, cos_table, sin_table,
@@ -29,111 +27,33 @@ def tile_attentioncore_pa_kernel(tc, x, qkv_kernel, qkv_bias, cos_table, sin_tab
     nc = tc.nc
     with ExitStack() as ctx:
         const = ctx.enter_context(tc.tile_pool(name="const", bufs=1))
-        rawp = ctx.enter_context(tc.tile_pool(name="rawp", bufs=2))
-        grpp = ctx.enter_context(tc.tile_pool(name="grpp", bufs=6))
+        rawp = ctx.enter_context(tc.tile_pool(name="rawp", bufs=4))
+        grps = ctx.enter_context(tc.tile_pool(name="grps", bufs=4))
+        grpv = ctx.enter_context(tc.tile_pool(name="grpv", bufs=1))
+        grpg = ctx.enter_context(tc.tile_pool(name="grpg", bufs=1))
+        vop = ctx.enter_context(tc.tile_pool(name="vop", bufs=3))
         codes = ctx.enter_context(tc.tile_pool(name="codes", bufs=1))
         tup = ctx.enter_context(tc.tile_pool(name="tup", bufs=4))
-        outp = ctx.enter_context(tc.tile_pool(name="outp", bufs=3))
+        outp = ctx.enter_context(tc.tile_pool(name="outp", bufs=2))
         accp = ctx.enter_context(tc.psum_pool(name="accp", bufs=4))
-        trp = ctx.enter_context(tc.psum_pool(name="trp", bufs=4))
-        ctx.enter_context(tc.manual_schedule(engines={mybir.EngineType.PE}))
+        psp = ctx.enter_context(tc.psum_pool(name="psp", bufs=4))
+        ctx.enter_context(tc.manual_schedule())
 
         cos_sb = const.tile([P, 4, 32], BF16, name="cos_sb", tag="cos_sb")
         sin_sb = const.tile([P, 4, 32], BF16, name="sin_sb", tag="sin_sb")
         b2d = const.tile([P, P], BF16, name="b2d", tag="b2d")
-        nc.vector.memset(b2d[:], 0.0)
-        nc.scalar.dma_start(out=cos_sb[:], in_=cos_table.rearrange("(i p) j -> p i j", p=P))
-        nc.scalar.dma_start(out=sin_sb[:], in_=sin_table.rearrange("(i p) j -> p i j", p=P))
-        nc.scalar.dma_start(out=b2d[0:24, :], in_=qkv_bias.rearrange("(r c) -> r c", c=P))
-
         x_sb = const.tile([P, 4, H], BF16, name="x_sb", tag="x_sb")
-        for i in range(4):
-            nc.sync.dma_start(out=x_sb[:, i, :], in_=x[i * P:(i + 1) * P, :])
-        raw01 = rawp.tile([P, 2, NG, 4, GW], BF16, name="raw01", tag="raw")
-        for n in range(2):
-            for g in range(NG):
-                nc.sync.dma_start(
-                    out=raw01[:, n, g, :, :],
-                    in_=qkv_kernel[g * 512:(g + 1) * 512, n * GW:(n + 1) * GW].rearrange(
-                        "(p j) w -> p j w", j=4))
-        raw_wide = []
-        for h in range(2):
-            rw = rawp.tile([P, NG, 4, 2 * GW], BF16, name="raww%d" % h, tag="raw")
-            for g in range(NG):
-                nc.sync.dma_start(
-                    out=rw[:, g, :, :],
-                    in_=qkv_kernel[g * 512:(g + 1) * 512,
-                                   (2 + 2 * h) * GW:(4 + 2 * h) * GW].rearrange(
-                        "(p j) w -> p j w", j=4))
-            raw_wide.append(rw)
-
-        def raw_unit(n, g):
-            if n < 2:
-                return raw01[:, n, g, :, :]
-            return raw_wide[(n - 2) // 2][:, g, :, (n % 2) * GW:(n % 2 + 1) * GW]
-
         ident_f = const.tile([P, P], F32, name="ident_f", tag="ident_f")
-        make_identity(nc, ident_f[:])
         ident_b = const.tile([P, P], BF16, name="ident_b", tag="ident_b")
-        nc.vector.tensor_copy(out=ident_b[:], in_=ident_f[:])
         perm_f = const.tile([P, P], F32, name="perm_f", tag="perm_f")
-        pv = perm_f[:].rearrange("p (a h j) -> p a h j", a=2, h=2)
-        iv = ident_f[:].rearrange("p (a h j) -> p a h j", a=2, h=2)
-        nc.vector.tensor_copy(out=pv[:, :, 0, :], in_=iv[:, :, 1, :])
-        nc.vector.tensor_copy(out=pv[:, :, 1, :], in_=iv[:, :, 0, :])
-
         e_c = const.tile([P, 4, P], BF16, name="e_c", tag="e_c")
         e_s = const.tile([P, 4, P], BF16, name="e_s", tag="e_s")
-        for r in range(4):
-            nc.vector.tensor_copy(out=e_c[:, :, r * 32:(r + 1) * 32], in_=cos_sb[:])
-            if r % 2 == 0:
-                nc.vector.tensor_copy(out=e_s[:, :, r * 32:(r + 1) * 32], in_=sin_sb[:])
-            else:
-                nc.vector.tensor_scalar_mul(out=e_s[:, :, r * 32:(r + 1) * 32], in0=sin_sb[:],
-                                            scalar1=-1.0)
         ct = const.tile([P, S_TOK], BF16, name="ct", tag="ct")
         snt = const.tile([P, S_TOK], BF16, name="snt", tag="snt")
-        for (src, dst, nm) in ((e_c, ct, "ctp"), (e_s, snt, "sntp")):
-            tb = accp.tile([P, S_TOK], BF16, name=nm, tag="acc")
-            for i in range(4):
-                nc.tensor.transpose(tb[:, i * P:(i + 1) * P], src[:, i, :], ident_b[:])
-            nc.vector.tensor_copy(out=dst[:], in_=tb[:])
         b_pp = const.tile([P, P], F32, name="b_pp", tag="b_pp")
-        btp = accp.tile([P, P], BF16, name="btp", tag="acc")
-        nc.tensor.transpose(btp[:], b2d[:], ident_b[:])
-        nc.vector.tensor_copy(out=b_pp[:], in_=btp[:])
         bv_bc = const.tile([P, GW], F32, name="bv_bc", tag="bv_bc")
-        bvp = accp.tile([P, GW], F32, name="bvp", tag="acc")
-        for r in range(4):
-            nc.tensor.matmul(out=bvp[:, r * P:(r + 1) * P],
-                             lhsT=ident_b[:, 20 + r:21 + r].to_broadcast([P, P]),
-                             rhs=b2d[:], start=True, stop=True)
-        nc.vector.tensor_copy(out=bv_bc[:], in_=bvp[:])
-
         xc = codes.tile([P, NG, S_TOK], U32, name="xc", tag="xc", align_bytes=64)
         xs = codes.tile([P, NG, S_TOK], U8, name="xs", tag="xs", align_bytes=64)
-        gxs = []
-        for g in range(NG):
-            gx = grpp.tile([P, 4 * S_TOK], BF16, name="gx%d" % g, tag="grp", align_bytes=64)
-            gxs.append(gx)
-        for ip in range(2):
-            for g in range(NG):
-                xt = trp.tile([P, 2, 2, P], F32, name="xt%d%d" % (ip, g), tag="tr")
-                for a in range(2):
-                    words = x_sb[:, 2 * ip + a, :].bitcast(F32)
-                    for u in range(2):
-                        nc.tensor.transpose(xt[:, a, u, :],
-                                            words[:, 256 * g + u:256 * (g + 1):2], ident_f[:])
-                dst = gxs[g][:].bitcast(F32).rearrange("p (i r u) -> p i r u", i=4, u=2)
-                src = xt[:].rearrange("p a u r -> p a r u")
-                if g % 2 == 0:
-                    nc.scalar.copy(out=dst[:, 2 * ip:2 * ip + 2, :, :], in_=src)
-                else:
-                    nc.vector.tensor_copy(out=dst[:, 2 * ip:2 * ip + 2, :, :], in_=src)
-
-        def quant_x(g):
-            nc.vector.quantize_mx(out=xc[:, g, :].bitcast(E5X4), scales=xs[:, g, :], in_=gxs[g][:])
-
         wcs = []
         wss = []
         for n in range(NGRP):
@@ -141,18 +61,130 @@ def tile_attentioncore_pa_kernel(tc, x, qkv_kernel, qkv_bias, cos_table, sin_tab
             ws = codes.tile([P, NG, GW], U8, name="ws%d" % n, tag="ws%d" % n, align_bytes=64)
             wcs.append(wc)
             wss.append(ws)
+        raws = {}
+        gxs = {}
         grs = {}
+        pst = {}
+        accs = {}
+        tts = {}
+        uts = {}
+        outs = {}
+        vos = {}
+        q3 = out_0.rearrange("s h d -> s (h d)").rearrange("(i p) c -> p i c", p=P)
+        k3 = out_1.rearrange("s h d -> s (h d)").rearrange("(i p) c -> p i c", p=P)
+        v2 = out_2.rearrange("s h d -> s (h d)")
 
-        def copy_unit(n, g):
-            gr = grpp.tile([P, 4 * GW], BF16, name="gr%d%d" % (n, g), tag="grp", align_bytes=64)
-            grs[(n, g)] = gr
-            if PAT_B:
-                dst = gr[:].rearrange("p (c i j) -> p c j i", i=4, j=4)
-                src = raw_unit(n, g).rearrange("p j (c i) -> p c j i", i=4)
+        def load_tabs():
+            nc.sync.dma_start(out=cos_sb[:], in_=cos_table.rearrange("(i p) j -> p i j", p=P))
+            nc.sync.dma_start(out=sin_sb[:], in_=sin_table.rearrange("(i p) j -> p i j", p=P))
+
+        def load_bias():
+            nc.sync.dma_start(out=b2d[0:24, :], in_=qkv_bias.rearrange("(r c) -> r c", c=P))
+
+        def load_x(i):
+            nc.sync.dma_start(out=x_sb[:, i, :], in_=x[i * P:(i + 1) * P, :])
+
+        def load_w(n, g):
+            if n not in raws:
+                raw_new = rawp.tile([P, NG, 4, GW], BF16, name="raw%d" % n, tag="raw")
+                raws[n] = raw_new
+            nc.sync.dma_start(
+                out=raws[n][:, g, :, :],
+                in_=qkv_kernel[g * 512:(g + 1) * 512, n * GW:(n + 1) * GW].rearrange(
+                    "(p j) w -> p j w", j=4))
+
+        def make_ident():
+            make_identity(nc, ident_f[:])
+
+        def consts_v():
+            nc.vector.tensor_copy(out=ident_b[:], in_=ident_f[:])
+            pv = perm_f[:].rearrange("p (a h j) -> p a h j", a=2, h=2)
+            iv = ident_f[:].rearrange("p (a h j) -> p a h j", a=2, h=2)
+            nc.vector.tensor_copy(out=pv[:, :, 0, :], in_=iv[:, :, 1, :])
+            nc.vector.tensor_copy(out=pv[:, :, 1, :], in_=iv[:, :, 0, :])
+
+        def tables_v():
+            for r in range(4):
+                nc.vector.tensor_copy(out=e_c[:, :, r * 32:(r + 1) * 32], in_=cos_sb[:])
+                if r % 2 == 0:
+                    nc.vector.tensor_copy(out=e_s[:, :, r * 32:(r + 1) * 32], in_=sin_sb[:])
+                else:
+                    nc.vector.tensor_scalar_mul(out=e_s[:, :, r * 32:(r + 1) * 32], in0=sin_sb[:],
+                                                scalar1=-1.0)
+
+        def table_pe(i):
+            if i < 2:
+                tb = psp.tile([P, S_TOK], BF16, name="tb%d" % i, tag="ps")
+                src = (e_c, e_s)[i]
+                for b in range(4):
+                    nc.tensor.transpose(tb[:, b * P:(b + 1) * P], src[:, b, :], ident_b[:])
+            elif i == 2:
+                tb = psp.tile([P, P], BF16, name="tb2", tag="ps")
+                nc.tensor.transpose(tb[:], b2d[:], ident_b[:])
             else:
-                dst = gr[:].rearrange("p (w j) -> p w j", j=4)
-                src = raw_unit(n, g).rearrange("p j w -> p w j")
-            eng = ASG[n][g]
+                tb = psp.tile([P, GW], F32, name="tb3", tag="ps")
+                for r in range(4):
+                    nc.tensor.matmul(out=tb[:, r * P:(r + 1) * P],
+                                     lhsT=ident_b[:, 20 + r:21 + r].to_broadcast([P, P]),
+                                     rhs=b2d[:], start=True, stop=True)
+            pst[("tb", i)] = tb
+
+        def table_out(i):
+            nc.scalar.copy(out=(ct, snt, b_pp, bv_bc)[i][:], in_=pst[("tb", i)][:])
+
+        def x_turn(ip, g):
+            xt = psp.tile([P, 2, 2, P], F32, name="xt%d%d" % (ip, g), tag="ps")
+            pst[("xt", ip, g)] = xt
+            for a in range(2):
+                words = x_sb[:, 2 * ip + a, :].bitcast(F32)
+                for u in range(2):
+                    nc.tensor.transpose(xt[:, a, u, :], words[:, 256 * g + u:256 * (g + 1):2],
+                                        ident_f[:])
+
+        def x_out(ip, g, eng):
+            if g // 2 not in gxs:
+                gx = outp.tile([P, 2, 4 * S_TOK], BF16, name="gx%d" % (g // 2), tag="o", align_bytes=64)
+                gxs[g // 2] = gx
+            dst = gxs[g // 2][:, g % 2, :].bitcast(F32).rearrange("p (i r u) -> p i r u", i=4, u=2)
+            src = pst[("xt", ip, g)][:].rearrange("p a u r -> p a r u")
+            if eng == "V":
+                nc.vector.tensor_copy(out=dst[:, 2 * ip:2 * ip + 2, :, :], in_=src)
+            else:
+                nc.scalar.copy(out=dst[:, 2 * ip:2 * ip + 2, :, :], in_=src)
+
+        def quant_x(g):
+            nc.vector.quantize_mx(out=xc[:, g, :].bitcast(E5X4), scales=xs[:, g, :],
+                                  in_=gxs[g // 2][:, g % 2, :])
+
+        def group_tile(n, g, eng):
+            if (n, g) not in grs:
+                if eng == "S":
+                    gr = grps.tile([P, 4 * GW], BF16, name="gr%d%d" % (n, g), tag="grs", align_bytes=64)
+                    grs[(n, g)] = gr[:]
+                elif eng == "V":
+                    gr = grpv.tile([P, 4 * GW], BF16, name="gr%d%d" % (n, g), tag="grv", align_bytes=64)
+                    grs[(n, g)] = gr[:]
+                else:
+                    pair = G_UNITS[n]
+                    gr = grpg.tile([P, 2, 4 * GW], BF16, name="grg%d" % n, tag="grg", align_bytes=64)
+                    grs[(n, pair[0])] = gr[:, 0, :]
+                    grs[(n, pair[1])] = gr[:, 1, :]
+            return grs[(n, g)]
+
+        def copy_unit(n, g, eng):
+            interleave(group_tile(n, g, eng), raws[n][:, g, :, :], eng)
+
+        def copy_half(n, g, h, eng):
+            gr = group_tile(n, g, "G")
+            interleave(gr[:, h * 2 * GW:(h + 1) * 2 * GW], raws[n][:, g, :, h * 256:(h + 1) * 256], eng)
+
+        def interleave(gr, raw, eng):
+            if PAT_B and eng != "G":
+                dst = gr.rearrange("p (c i j) -> p c j i", i=4, j=4)
+                src = raw.rearrange("p j (c i) -> p c j i", i=4)
+            else:
+                dst = gr.rearrange("p (w j) -> p w j", j=4)
+                src = raw.rearrange("p j w -> p w j")
             if eng == "V":
                 nc.vector.tensor_copy(out=dst, in_=src)
             elif eng == "S":
@@ -162,16 +194,7 @@ def tile_attentioncore_pa_kernel(tc, x, qkv_kernel, qkv_bias, cos_table, sin_tab
 
         def quant_unit(n, g):
             nc.vector.quantize_mx(out=wcs[n][:, g, :].bitcast(E5X4), scales=wss[n][:, g, :],
-                                  in_=grs[(n, g)][:])
-
-        q3 = out_0.rearrange("s h d -> s (h d)").rearrange("(i p) c -> p i c", p=P)
-        k3 = out_1.rearrange("s h d -> s (h d)").rearrange("(i p) c -> p i c", p=P)
-        v2 = out_2.rearrange("s h d -> s (h d)")
-
-        accs = {}
-        tus = {}
-        trs = {}
-        outs = {}
+                                  in_=grs[(n, g)])
 
         def mx(m, g):
             if g == 0:
@@ -191,77 +214,358 @@ def tile_attentioncore_pa_kernel(tc, x, qkv_kernel, qkv_bias, cos_table, sin_tab
                                     rhs=wcs[5][:, g, :].bitcast(E5X4), rhs_scale=wss[5][:, g, :],
                                     start=(g == 0), stop=(g == NG - 1))
 
-        def rot(m):
+        def rot_t(m):
             t_t = tup.tile([P, S_TOK], F32, name="t%d" % m, tag="t")
-            u_t = tup.tile([P, S_TOK], F32, name="u%d" % m, tag="u")
-            tus[m] = (t_t, u_t)
+            tts[m] = t_t
             nc.vector.scalar_tensor_tensor(out=t_t[:], in0=accs[m][:], scalar=b_pp[:, m:m + 1],
                                            in1=ct[:], op0=ADD, op1=MULT)
+
+        def rot_u(m):
+            u_t = tup.tile([P, S_TOK], F32, name="u%d" % m, tag="u")
+            uts[m] = u_t
             nc.vector.scalar_tensor_tensor(out=u_t[:], in0=accs[m][:], scalar=b_pp[:, m:m + 1],
                                            in1=snt[:], op0=ADD, op1=MULT)
 
         def back(m):
-            tr = trp.tile([P, 4, P], F32, name="tr%d" % m, tag="tr")
-            trs[m] = tr
-            (t_t, u_t) = tus[m]
+            tr = psp.tile([P, 4, P], F32, name="tr%d" % m, tag="ps")
+            pst[("tr", m)] = tr
             for i in range(4):
-                nc.tensor.matmul(out=tr[:, i, :], lhsT=t_t[:, i * P:(i + 1) * P], rhs=ident_f[:],
+                nc.tensor.matmul(out=tr[:, i, :], lhsT=tts[m][:, i * P:(i + 1) * P], rhs=ident_f[:],
                                  is_transpose=True, start=True, stop=False)
-                nc.tensor.matmul(out=tr[:, i, :], lhsT=u_t[:, i * P:(i + 1) * P], rhs=perm_f[:],
+                nc.tensor.matmul(out=tr[:, i, :], lhsT=uts[m][:, i * P:(i + 1) * P], rhs=perm_f[:],
                                  is_transpose=True, start=False, stop=True)
 
         def leave(m):
             n = m // 4
-            if m % 4 == 0:
-                o_new = outp.tile([P, 4, GW], F32, name="o%d" % n, tag="o")
+            if n not in outs:
+                o_new = outp.tile([P, 4, GW], F32, name="o%d" % n, tag="o", align_bytes=64)
                 outs[n] = o_new
-            nc.scalar.copy(out=outs[n][:, :, (m % 4) * P:(m % 4 + 1) * P], in_=trs[m][:])
-            if m % 4 == 3:
-                if n < 4:
-                    nc.scalar.dma_start(out=q3[:, :, n * GW:(n + 1) * GW], in_=outs[n][:])
-                else:
-                    nc.scalar.dma_start(out=k3, in_=outs[n][:])
+            nc.scalar.copy(out=outs[n][:, :, (m % 4) * P:(m % 4 + 1) * P], in_=pst[("tr", m)][:])
+
+        def store_q(n):
+            nc.scalar.dma_start(out=q3[:, :, n * GW:(n + 1) * GW], in_=outs[n][:])
+
+        def store_k(h):
+            half = slice(h * 2 * P, (h + 1) * 2 * P)
+            nc.scalar.dma_start(out=k3[:, :, half], in_=outs[4][:, :, half])
 
         def v_out(i):
-            vo = outp.tile([P, GW], F32, name="vo%d" % i, tag="vo")
+            vo = vop.tile([P, GW], F32, name="vo%d" % i, tag="vo")
+            vos[i] = vo
             nc.vector.tensor_tensor(out=vo[:], in0=accs[20 + i][:], in1=bv_bc[:], op=ADD)
-            nc.sync.dma_start(out=v2[i * P:(i + 1) * P, :], in_=vo[:])
 
-        for g in range(NG):
-            copy_unit(0, g)
-            quant_x(g)
-            quant_unit(0, g)
-            for m in range(4):
-                mx(m, g)
-        units = [(n, g) for n in range(1, NGRP) for g in range(NG)]
-        todo_c = list(units)
-        todo_q = list(units)
+        def v_store(i):
+            nc.sync.dma_start(out=v2[i * P:(i + 1) * P, :], in_=vos[i][:])
 
-        def copies(cnt):
-            for (n, g) in todo_c[:cnt]:
-                copy_unit(n, g)
-            todo_c[:cnt] = []
-
-        def quants(cnt):
-            for (n, g) in todo_q[:cnt]:
-                quant_unit(n, g)
-            todo_q[:cnt] = []
-
-        copies(LOOKAHEAD)
-        for k in range(12):
-            if 1 <= k <= 10:
-                for m in (2 * k + 2, 2 * k + 3):
-                    for g in range(NG):
-                        mx(m, g)
-            for m in (2 * k, 2 * k + 1):
-                if k < 10:
-                    rot(m)
-                else:
-                    v_out(m - 20)
-            if k < 10:
-                back(2 * k)
-                back(2 * k + 1)
-                leave(2 * k)
-                leave(2 * k + 1)
-            quants(4 if k == 0 else 2)
-            copies(2)
+        nc.gpsimd.memset(b2d[:], 0.0)
+        load_tabs()
+        load_w(0, 0)
+        load_w(0, 1)
+        load_x(0)
+        load_x(1)
+        load_x(2)
+        load_x(3)
+        load_bias()
+        load_w(0, 2)
+        load_w(0, 3)
+        load_w(1, 0)
+        load_w(1, 1)
+        load_w(1, 2)
+        load_w(1, 3)
+        load_w(2, 0)
+        load_w(2, 1)
+        load_w(2, 2)
+        load_w(2, 3)
+        load_w(3, 0)
+        load_w(3, 1)
+        load_w(3, 2)
+        load_w(3, 3)
+        load_w(4, 0)
+        load_w(4, 1)
+        load_w(4, 2)
+        load_w(4, 3)
+        load_w(5, 0)
+        load_w(5, 1)
+        load_w(5, 2)
+        load_w(5, 3)
+        make_ident()
+        consts_v()
+        tables_v()
+        table_pe(0)
+        table_out(0)
+        table_pe(1)
+        table_out(1)
+        table_pe(2)
+        table_out(2)
+        table_pe(3)
+        table_out(3)
+        copy_half(0, 0, 0, "G")
+        copy_half(0, 0, 1, "G")
+        copy_half(0, 1, 0, "G")
+        copy_half(0, 1, 1, "G")
+        quant_unit(0, 0)
+        quant_unit(0, 1)
+        x_turn(0, 0)
+        x_out(0, 0, "S")
+        x_turn(0, 1)
+        x_out(0, 1, "S")
+        x_turn(0, 2)
+        x_out(0, 2, "S")
+        x_turn(0, 3)
+        x_out(0, 3, "S")
+        x_turn(1, 0)
+        x_out(1, 0, "S")
+        x_turn(1, 1)
+        x_out(1, 1, "S")
+        x_turn(1, 2)
+        x_out(1, 2, "S")
+        x_turn(1, 3)
+        x_out(1, 3, "S")
+        copy_unit(0, 2, "S")
+        quant_x(0)
+        quant_x(1)
+        mx(0, 0)
+        mx(1, 0)
+        mx(2, 0)
+        mx(3, 0)
+        quant_x(2)
+        mx(0, 1)
+        mx(1, 1)
+        mx(2, 1)
+        mx(3, 1)
+        quant_x(3)
+        copy_unit(0, 3, "V")
+        quant_unit(0, 2)
+        mx(0, 2)
+        mx(1, 2)
+        mx(2, 2)
+        mx(3, 2)
+        quant_unit(0, 3)
+        mx(0, 3)
+        mx(1, 3)
+        mx(2, 3)
+        mx(3, 3)
+        copy_unit(1, 0, "S")
+        copy_unit(1, 2, "S")
+        copy_half(1, 1, 0, "G")
+        copy_half(1, 1, 1, "G")
+        copy_half(1, 3, 0, "G")
+        rot_t(0)
+        rot_u(0)
+        rot_t(1)
+        rot_u(1)
+        copy_half(1, 3, 1, "V")
+        quant_unit(1, 0)
+        quant_unit(1, 2)
+        quant_unit(1, 1)
+        quant_unit(1, 3)
+        copy_half(2, 1, 0, "G")
+        copy_half(2, 1, 1, "G")
+        copy_half(2, 3, 0, "G")
+        back(0)
+        back(1)
+        copy_unit(2, 0, "S")
+        leave(0)
+        leave(1)
+        mx(4, 0)
+        mx(5, 0)
+        mx(4, 1)
+        mx(5, 1)
+        mx(4, 2)
+        mx(5, 2)
+        mx(4, 3)
+        mx(5, 3)
+        rot_t(2)
+        rot_u(2)
+        rot_t(3)
+        rot_u(3)
+        back(2)
+        back(3)
+        copy_unit(2, 2, "S")
+        leave(2)
+        leave(3)
+        store_q(0)
+        mx(6, 0)
+        mx(6, 1)
+        mx(6, 2)
+        mx(6, 3)
+        mx(7, 0)
+        mx(7, 1)
+        mx(7, 2)
+        mx(7, 3)
+        rot_t(4)
+        rot_u(4)
+        rot_t(5)
+        rot_u(5)
+        copy_half(2, 3, 1, "V")
+        quant_unit(2, 0)
+        quant_unit(2, 2)
+        quant_unit(2, 1)
+        quant_unit(2, 3)
+        copy_half(3, 1, 0, "G")
+        copy_half(3, 1, 1, "G")
+        copy_half(3, 3, 0, "G")
+        back(4)
+        back(5)
+        copy_unit(3, 0, "S")
+        leave(4)
+        leave(5)
+        mx(8, 0)
+        mx(8, 1)
+        mx(8, 2)
+        mx(8, 3)
+        mx(9, 0)
+        mx(9, 1)
+        mx(9, 2)
+        mx(9, 3)
+        rot_t(6)
+        rot_u(6)
+        rot_t(7)
+        rot_u(7)
+        back(6)
+        back(7)
+        copy_unit(3, 2, "S")
+        leave(6)
+        leave(7)
+        store_q(1)
+        mx(10, 0)
+        mx(10, 1)
+        mx(10, 2)
+        mx(10, 3)
+        mx(11, 0)
+        mx(11, 1)
+        mx(11, 2)
+        mx(11, 3)
+        rot_t(8)
+        rot_u(8)
+        rot_t(9)
+        rot_u(9)
+        copy_half(3, 3, 1, "V")
+        quant_unit(3, 0)
+        quant_unit(3, 2)
+        quant_unit(3, 1)
+        quant_unit(3, 3)
+        copy_half(4, 1, 0, "G")
+        copy_half(4, 1, 1, "G")
+        copy_half(4, 3, 0, "G")
+        back(8)
+        back(9)
+        copy_unit(4, 0, "S")
+        leave(8)
+        leave(9)
+        mx(12, 0)
+        mx(12, 1)
+        mx(12, 2)
+        mx(12, 3)
+        mx(13, 0)
+        mx(13, 1)
+        mx(13, 2)
+        mx(13, 3)
+        rot_t(10)
+        rot_u(10)
+        rot_t(11)
+        rot_u(11)
+        back(10)
+        back(11)
+        copy_unit(4, 2, "S")
+        leave(10)
+        leave(11)
+        store_q(2)
+        mx(14, 0)
+        mx(14, 1)
+        mx(14, 2)
+        mx(14, 3)
+        mx(15, 0)
+        mx(15, 1)
+        mx(15, 2)
+        mx(15, 3)
+        rot_t(12)
+        rot_u(12)
+        rot_t(13)
+        rot_u(13)
+        copy_half(4, 3, 1, "V")
+        quant_unit(4, 0)
+        quant_unit(4, 2)
+        quant_unit(4, 1)
+        quant_unit(4, 3)
+        copy_half(5, 1, 0, "G")
+        copy_half(5, 1, 1, "G")
+        copy_half(5, 3, 0, "G")
+        back(12)
+        back(13)
+        copy_unit(5, 0, "S")
+        leave(12)
+        leave(13)
+        mx(16, 0)
+        mx(16, 1)
+        mx(16, 2)
+        mx(16, 3)
+        mx(17, 0)
+        mx(17, 1)
+        mx(17, 2)
+        mx(17, 3)
+        rot_t(14)
+        rot_u(14)
+        rot_t(15)
+        rot_u(15)
+        back(14)
+        back(15)
+        copy_unit(5, 2, "S")
+        leave(14)
+        leave(15)
+        store_q(3)
+        mx(18, 0)
+        mx(18, 1)
+        mx(18, 2)
+        mx(18, 3)
+        mx(19, 0)
+        mx(19, 1)
+        mx(19, 2)
+        mx(19, 3)
+        rot_t(16)
+        rot_u(16)
+        rot_t(17)
+        rot_u(17)
+        copy_half(5, 3, 1, "V")
+        quant_unit(5, 0)
+        quant_unit(5, 2)
+        quant_unit(5, 1)
+        quant_unit(5, 3)
+        back(16)
+        back(17)
+        leave(16)
+        leave(17)
+        store_k(0)
+        mx(20, 0)
+        mx(20, 1)
+        mx(20, 2)
+        mx(20, 3)
+        mx(21, 0)
+        mx(21, 1)
+        mx(21, 2)
+        mx(21, 3)
+        rot_t(18)
+        rot_u(18)
+        rot_t(19)
+        rot_u(19)
+        back(18)
+        back(19)
+        leave(18)
+        leave(19)
+        store_k(1)
+        mx(22, 0)
+        mx(22, 1)
+        mx(22, 2)
+        mx(22, 3)
+        mx(23, 0)
+        mx(23, 1)
+        mx(23, 2)
+        mx(23, 3)
+        v_out(0)
+        v_store(0)
+        v_out(1)
+        v_store(1)
+        v_out(2)
+        v_store(2)
+        v_out(3)
+        v_store(3)

@@ -178,6 +178,10 @@ def tile_attentioncore_pa_kernel(tc, x, qkv_kernel, qkv_bias, cos_table, sin_tab
             gr = group_tile(n, g, "G")
             interleave(gr[:, h * 2 * GW:(h + 1) * 2 * GW], raws[n][:, g, :, h * 256:(h + 1) * 256], eng)
 
+        def copy_part(n, g, q0, q1, eng):
+            gr = group_tile(n, g, "G")
+            interleave(gr[:, q0 * GW:q1 * GW], raws[n][:, g, :, q0 * P:q1 * P], eng)
+
         def interleave(gr, raw, eng):
             if PAT_B and eng != "G":
                 dst = gr.rearrange("p (c i j) -> p c j i", i=4, j=4)
@@ -299,10 +303,8 @@ def tile_attentioncore_pa_kernel(tc, x, qkv_kernel, qkv_bias, cos_table, sin_tab
         table_out(2)
         table_pe(3)
         table_out(3)
-        copy_half(0, 0, 0, "G")
-        copy_half(0, 0, 1, "G")
-        copy_half(0, 1, 0, "G")
-        copy_half(0, 1, 1, "G")
+        copy_unit(0, 0, "G")
+        copy_unit(0, 1, "G")
         quant_unit(0, 0)
         quant_unit(0, 1)
         x_turn(0, 0)
@@ -347,21 +349,18 @@ def tile_attentioncore_pa_kernel(tc, x, qkv_kernel, qkv_bias, cos_table, sin_tab
         mx(3, 3)
         copy_unit(1, 0, "S")
         copy_unit(1, 2, "S")
-        copy_half(1, 1, 0, "G")
-        copy_half(1, 1, 1, "G")
-        copy_half(1, 3, 0, "G")
+        copy_unit(1, 1, "G")
+        copy_part(1, 3, 0, 1, "S")
         rot_t(0)
         rot_u(0)
         rot_t(1)
         rot_u(1)
-        copy_half(1, 3, 1, "V")
+        copy_part(1, 3, 1, 4, "V")
         quant_unit(1, 0)
         quant_unit(1, 2)
         quant_unit(1, 1)
         quant_unit(1, 3)
-        copy_half(2, 1, 0, "G")
-        copy_half(2, 1, 1, "G")
-        copy_half(2, 3, 0, "G")
+        copy_unit(2, 1, "G")
         back(0)
         back(1)
         copy_unit(2, 0, "S")
@@ -382,6 +381,7 @@ def tile_attentioncore_pa_kernel(tc, x, qkv_kernel, qkv_bias, cos_table, sin_tab
         back(2)
         back(3)
         copy_unit(2, 2, "S")
+        copy_part(2, 3, 0, 1, "S")
         leave(2)
         leave(3)
         store_q(0)
@@ -397,14 +397,12 @@ def tile_attentioncore_pa_kernel(tc, x, qkv_kernel, qkv_bias, cos_table, sin_tab
         rot_u(4)
         rot_t(5)
         rot_u(5)
-        copy_half(2, 3, 1, "V")
+        copy_part(2, 3, 1, 4, "V")
         quant_unit(2, 0)
         quant_unit(2, 2)
         quant_unit(2, 1)
         quant_unit(2, 3)
-        copy_half(3, 1, 0, "G")
-        copy_half(3, 1, 1, "G")
-        copy_half(3, 3, 0, "G")
+        copy_unit(3, 1, "G")
         back(4)
         back(5)
         copy_unit(3, 0, "S")
@@ -425,6 +423,7 @@ def tile_attentioncore_pa_kernel(tc, x, qkv_kernel, qkv_bias, cos_table, sin_tab
         back(6)
         back(7)
         copy_unit(3, 2, "S")
+        copy_part(3, 3, 0, 1, "S")
         leave(6)
         leave(7)
         store_q(1)
@@ -440,14 +439,12 @@ def tile_attentioncore_pa_kernel(tc, x, qkv_kernel, qkv_bias, cos_table, sin_tab
         rot_u(8)
         rot_t(9)
         rot_u(9)
-        copy_half(3, 3, 1, "V")
+        copy_part(3, 3, 1, 4, "V")
         quant_unit(3, 0)
         quant_unit(3, 2)
         quant_unit(3, 1)
         quant_unit(3, 3)
-        copy_half(4, 1, 0, "G")
-        copy_half(4, 1, 1, "G")
-        copy_half(4, 3, 0, "G")
+        copy_unit(4, 1, "G")
         back(8)
         back(9)
         copy_unit(4, 0, "S")
@@ -468,6 +465,7 @@ def tile_attentioncore_pa_kernel(tc, x, qkv_kernel, qkv_bias, cos_table, sin_tab
         back(10)
         back(11)
         copy_unit(4, 2, "S")
+        copy_part(4, 3, 0, 1, "S")
         leave(10)
         leave(11)
         store_q(2)
@@ -483,14 +481,12 @@ def tile_attentioncore_pa_kernel(tc, x, qkv_kernel, qkv_bias, cos_table, sin_tab
         rot_u(12)
         rot_t(13)
         rot_u(13)
-        copy_half(4, 3, 1, "V")
+        copy_part(4, 3, 1, 4, "V")
         quant_unit(4, 0)
         quant_unit(4, 2)
         quant_unit(4, 1)
         quant_unit(4, 3)
-        copy_half(5, 1, 0, "G")
-        copy_half(5, 1, 1, "G")
-        copy_half(5, 3, 0, "G")
+        copy_unit(5, 1, "G")
         back(12)
         back(13)
         copy_unit(5, 0, "S")
@@ -511,6 +507,7 @@ def tile_attentioncore_pa_kernel(tc, x, qkv_kernel, qkv_bias, cos_table, sin_tab
         back(14)
         back(15)
         copy_unit(5, 2, "S")
+        copy_part(5, 3, 0, 1, "S")
         leave(14)
         leave(15)
         store_q(3)
@@ -526,7 +523,7 @@ def tile_attentioncore_pa_kernel(tc, x, qkv_kernel, qkv_bias, cos_table, sin_tab
         rot_u(16)
         rot_t(17)
         rot_u(17)
-        copy_half(5, 3, 1, "V")
+        copy_part(5, 3, 1, 4, "V")
         quant_unit(5, 0)
         quant_unit(5, 2)
         quant_unit(5, 1)

@@ -75,11 +75,11 @@ def tile_attentioncore_pa_kernel(tc, x, qkv_kernel, qkv_bias, cos_table, sin_tab
         v2 = out_2.rearrange("s h d -> s (h d)")
 
         def load_tabs():
-            nc.sync.dma_start(out=cos_sb[:], in_=cos_table.rearrange("(i p) j -> p i j", p=P))
-            nc.sync.dma_start(out=sin_sb[:], in_=sin_table.rearrange("(i p) j -> p i j", p=P))
+            nc.scalar.dma_start(out=cos_sb[:], in_=cos_table.rearrange("(i p) j -> p i j", p=P))
+            nc.scalar.dma_start(out=sin_sb[:], in_=sin_table.rearrange("(i p) j -> p i j", p=P))
 
         def load_bias():
-            nc.sync.dma_start(out=b2d[0:24, :], in_=qkv_bias.rearrange("(r c) -> r c", c=P))
+            nc.scalar.dma_start(out=b2d[0:24, :], in_=qkv_bias.rearrange("(r c) -> r c", c=P))
 
         def load_x(i):
             nc.sync.dma_start(out=x_sb[:, i, :], in_=x[i * P:(i + 1) * P, :])
@@ -178,10 +178,6 @@ def tile_attentioncore_pa_kernel(tc, x, qkv_kernel, qkv_bias, cos_table, sin_tab
             gr = group_tile(n, g, "G")
             interleave(gr[:, h * 2 * GW:(h + 1) * 2 * GW], raws[n][:, g, :, h * 256:(h + 1) * 256], eng)
 
-        def copy_part(n, g, q0, q1, eng):
-            gr = group_tile(n, g, "G")
-            interleave(gr[:, q0 * GW:q1 * GW], raws[n][:, g, :, q0 * P:q1 * P], eng)
-
         def interleave(gr, raw, eng):
             if PAT_B and eng != "G":
                 dst = gr.rearrange("p (c i j) -> p c j i", i=4, j=4)
@@ -263,13 +259,13 @@ def tile_attentioncore_pa_kernel(tc, x, qkv_kernel, qkv_bias, cos_table, sin_tab
 
         nc.gpsimd.memset(b2d[:], 0.0)
         load_tabs()
+        load_bias()
         load_w(0, 0)
         load_w(0, 1)
         load_x(0)
         load_x(1)
         load_x(2)
         load_x(3)
-        load_bias()
         load_w(0, 2)
         load_w(0, 3)
         load_w(1, 0)
@@ -350,17 +346,18 @@ def tile_attentioncore_pa_kernel(tc, x, qkv_kernel, qkv_bias, cos_table, sin_tab
         copy_unit(1, 0, "S")
         copy_unit(1, 2, "S")
         copy_unit(1, 1, "G")
-        copy_part(1, 3, 0, 1, "S")
+        copy_half(1, 3, 0, "G")
         rot_t(0)
         rot_u(0)
         rot_t(1)
         rot_u(1)
-        copy_part(1, 3, 1, 4, "V")
+        copy_half(1, 3, 1, "V")
         quant_unit(1, 0)
         quant_unit(1, 2)
         quant_unit(1, 1)
         quant_unit(1, 3)
         copy_unit(2, 1, "G")
+        copy_half(2, 3, 0, "G")
         back(0)
         back(1)
         copy_unit(2, 0, "S")
@@ -381,7 +378,6 @@ def tile_attentioncore_pa_kernel(tc, x, qkv_kernel, qkv_bias, cos_table, sin_tab
         back(2)
         back(3)
         copy_unit(2, 2, "S")
-        copy_part(2, 3, 0, 1, "S")
         leave(2)
         leave(3)
         store_q(0)
@@ -397,12 +393,13 @@ def tile_attentioncore_pa_kernel(tc, x, qkv_kernel, qkv_bias, cos_table, sin_tab
         rot_u(4)
         rot_t(5)
         rot_u(5)
-        copy_part(2, 3, 1, 4, "V")
+        copy_half(2, 3, 1, "V")
         quant_unit(2, 0)
         quant_unit(2, 2)
         quant_unit(2, 1)
         quant_unit(2, 3)
         copy_unit(3, 1, "G")
+        copy_half(3, 3, 0, "G")
         back(4)
         back(5)
         copy_unit(3, 0, "S")
@@ -423,7 +420,6 @@ def tile_attentioncore_pa_kernel(tc, x, qkv_kernel, qkv_bias, cos_table, sin_tab
         back(6)
         back(7)
         copy_unit(3, 2, "S")
-        copy_part(3, 3, 0, 1, "S")
         leave(6)
         leave(7)
         store_q(1)
@@ -439,12 +435,13 @@ def tile_attentioncore_pa_kernel(tc, x, qkv_kernel, qkv_bias, cos_table, sin_tab
         rot_u(8)
         rot_t(9)
         rot_u(9)
-        copy_part(3, 3, 1, 4, "V")
+        copy_half(3, 3, 1, "V")
         quant_unit(3, 0)
         quant_unit(3, 2)
         quant_unit(3, 1)
         quant_unit(3, 3)
         copy_unit(4, 1, "G")
+        copy_half(4, 3, 0, "G")
         back(8)
         back(9)
         copy_unit(4, 0, "S")
@@ -465,7 +462,6 @@ def tile_attentioncore_pa_kernel(tc, x, qkv_kernel, qkv_bias, cos_table, sin_tab
         back(10)
         back(11)
         copy_unit(4, 2, "S")
-        copy_part(4, 3, 0, 1, "S")
         leave(10)
         leave(11)
         store_q(2)
@@ -481,12 +477,13 @@ def tile_attentioncore_pa_kernel(tc, x, qkv_kernel, qkv_bias, cos_table, sin_tab
         rot_u(12)
         rot_t(13)
         rot_u(13)
-        copy_part(4, 3, 1, 4, "V")
+        copy_half(4, 3, 1, "V")
         quant_unit(4, 0)
         quant_unit(4, 2)
         quant_unit(4, 1)
         quant_unit(4, 3)
         copy_unit(5, 1, "G")
+        copy_half(5, 3, 0, "G")
         back(12)
         back(13)
         copy_unit(5, 0, "S")
@@ -507,7 +504,6 @@ def tile_attentioncore_pa_kernel(tc, x, qkv_kernel, qkv_bias, cos_table, sin_tab
         back(14)
         back(15)
         copy_unit(5, 2, "S")
-        copy_part(5, 3, 0, 1, "S")
         leave(14)
         leave(15)
         store_q(3)
@@ -523,7 +519,7 @@ def tile_attentioncore_pa_kernel(tc, x, qkv_kernel, qkv_bias, cos_table, sin_tab
         rot_u(16)
         rot_t(17)
         rot_u(17)
-        copy_part(5, 3, 1, 4, "V")
+        copy_half(5, 3, 1, "V")
         quant_unit(5, 0)
         quant_unit(5, 2)
         quant_unit(5, 1)

@@ -18,8 +18,6 @@ P = 128
 NG = 4
 NGRP = 6
 GW = 512
-G_UNITS = ((0, 1), (1, 3), (1, 3), (1, 3), (1, 3), (1, 3))
-PAT_B = True
 
 
 def tile_attentioncore_pa_kernel(tc, x, qkv_kernel, qkv_bias, cos_table, sin_table,
@@ -31,16 +29,13 @@ def tile_attentioncore_pa_kernel(tc, x, qkv_kernel, qkv_bias, cos_table, sin_tab
         grps = ctx.enter_context(tc.tile_pool(name="grps", bufs=4))
         grpv = ctx.enter_context(tc.tile_pool(name="grpv", bufs=1))
         grpg = ctx.enter_context(tc.tile_pool(name="grpg", bufs=1))
-        vop = ctx.enter_context(tc.tile_pool(name="vop", bufs=3))
+        vop = ctx.enter_context(tc.tile_pool(name="vop", bufs=2))
         codes = ctx.enter_context(tc.tile_pool(name="codes", bufs=1))
         tup = ctx.enter_context(tc.tile_pool(name="tup", bufs=4))
         outp = ctx.enter_context(tc.tile_pool(name="outp", bufs=2))
-        accp = ctx.enter_context(tc.psum_pool(name="accp", bufs=4))
-        psp = ctx.enter_context(tc.psum_pool(name="psp", bufs=4))
+        bank = ctx.enter_context(tc.psum_pool(name="bank", bufs=8))
         ctx.enter_context(tc.manual_schedule())
 
-        cos_sb = const.tile([P, 4, 32], BF16, name="cos_sb", tag="cos_sb")
-        sin_sb = const.tile([P, 4, 32], BF16, name="sin_sb", tag="sin_sb")
         b2d = const.tile([P, P], BF16, name="b2d", tag="b2d")
         x_sb = const.tile([P, 4, H], BF16, name="x_sb", tag="x_sb")
         ident_f = const.tile([P, P], F32, name="ident_f", tag="ident_f")
@@ -48,10 +43,9 @@ def tile_attentioncore_pa_kernel(tc, x, qkv_kernel, qkv_bias, cos_table, sin_tab
         perm_f = const.tile([P, P], F32, name="perm_f", tag="perm_f")
         e_c = const.tile([P, 4, P], BF16, name="e_c", tag="e_c")
         e_s = const.tile([P, 4, P], BF16, name="e_s", tag="e_s")
-        ct = const.tile([P, S_TOK], BF16, name="ct", tag="ct")
-        snt = const.tile([P, S_TOK], BF16, name="snt", tag="snt")
+        cs = const.tile([P, 2, S_TOK], BF16, name="cs", tag="cs")
         b_pp = const.tile([P, P], F32, name="b_pp", tag="b_pp")
-        bv_bc = const.tile([P, GW], F32, name="bv_bc", tag="bv_bc")
+        bv_bc = const.tile([P, GW], BF16, name="bv_bc", tag="bv_bc")
         xc = codes.tile([P, NG, S_TOK], U32, name="xc", tag="xc", align_bytes=64)
         xs = codes.tile([P, NG, S_TOK], U8, name="xs", tag="xs", align_bytes=64)
         wcs = []
@@ -64,10 +58,8 @@ def tile_attentioncore_pa_kernel(tc, x, qkv_kernel, qkv_bias, cos_table, sin_tab
         raws = {}
         gxs = {}
         grs = {}
-        pst = {}
-        accs = {}
-        tts = {}
-        uts = {}
+        bks = {}
+        tus = {}
         outs = {}
         vos = {}
         q3 = out_0.rearrange("s h d -> s (h d)").rearrange("(i p) c -> p i c", p=P)
@@ -75,10 +67,8 @@ def tile_attentioncore_pa_kernel(tc, x, qkv_kernel, qkv_bias, cos_table, sin_tab
         v2 = out_2.rearrange("s h d -> s (h d)")
 
         def load_tabs():
-            nc.scalar.dma_start(out=cos_sb[:], in_=cos_table.rearrange("(i p) j -> p i j", p=P))
-            nc.scalar.dma_start(out=sin_sb[:], in_=sin_table.rearrange("(i p) j -> p i j", p=P))
-
-        def load_bias():
+            nc.scalar.dma_start(out=e_c[:, :, 0:32], in_=cos_table.rearrange("(i p) j -> p i j", p=P))
+            nc.scalar.dma_start(out=e_s[:, :, 0:32], in_=sin_table.rearrange("(i p) j -> p i j", p=P))
             nc.scalar.dma_start(out=b2d[0:24, :], in_=qkv_bias.rearrange("(r c) -> r c", c=P))
 
         def load_x(i):
@@ -93,9 +83,6 @@ def tile_attentioncore_pa_kernel(tc, x, qkv_kernel, qkv_bias, cos_table, sin_tab
                 in_=qkv_kernel[g * 512:(g + 1) * 512, n * GW:(n + 1) * GW].rearrange(
                     "(p j) w -> p j w", j=4))
 
-        def make_ident():
-            make_identity(nc, ident_f[:])
-
         def consts_v():
             nc.vector.tensor_copy(out=ident_b[:], in_=ident_f[:])
             pv = perm_f[:].rearrange("p (a h j) -> p a h j", a=2, h=2)
@@ -104,82 +91,74 @@ def tile_attentioncore_pa_kernel(tc, x, qkv_kernel, qkv_bias, cos_table, sin_tab
             nc.vector.tensor_copy(out=pv[:, :, 1, :], in_=iv[:, :, 0, :])
 
         def tables_v():
-            for r in range(4):
-                nc.vector.tensor_copy(out=e_c[:, :, r * 32:(r + 1) * 32], in_=cos_sb[:])
-                if r % 2 == 0:
-                    nc.vector.tensor_copy(out=e_s[:, :, r * 32:(r + 1) * 32], in_=sin_sb[:])
-                else:
-                    nc.vector.tensor_scalar_mul(out=e_s[:, :, r * 32:(r + 1) * 32], in0=sin_sb[:],
-                                                scalar1=-1.0)
+            nc.vector.tensor_copy(out=e_c[:, :, 32:64], in_=e_c[:, :, 0:32])
+            nc.vector.tensor_scalar_mul(out=e_s[:, :, 32:64], in0=e_s[:, :, 0:32], scalar1=-1.0)
+            nc.vector.tensor_copy(out=e_c[:, :, 64:128], in_=e_c[:, :, 0:64])
+            nc.vector.tensor_copy(out=e_s[:, :, 64:128], in_=e_s[:, :, 0:64])
 
-        def table_pe(i):
-            if i < 2:
-                tb = psp.tile([P, S_TOK], BF16, name="tb%d" % i, tag="ps")
-                src = (e_c, e_s)[i]
+        def new_bank(key, shape, dtype):
+            bk = bank.tile(shape, dtype, name="bk_%s" % key, tag="bk")
+            bks[key] = bk
+            return bk
+
+        def table_pe():
+            tb = new_bank("tb0", [P, 2, S_TOK], BF16)
+            for i in range(2):
                 for b in range(4):
-                    nc.tensor.transpose(tb[:, b * P:(b + 1) * P], src[:, b, :], ident_b[:])
-            elif i == 2:
-                tb = psp.tile([P, P], BF16, name="tb2", tag="ps")
-                nc.tensor.transpose(tb[:], b2d[:], ident_b[:])
-            else:
-                tb = psp.tile([P, GW], F32, name="tb3", tag="ps")
-                for r in range(4):
-                    nc.tensor.matmul(out=tb[:, r * P:(r + 1) * P],
-                                     lhsT=ident_b[:, 20 + r:21 + r].to_broadcast([P, P]),
-                                     rhs=b2d[:], start=True, stop=True)
-            pst[("tb", i)] = tb
+                    nc.tensor.transpose(tb[:, i, b * P:(b + 1) * P], (e_c, e_s)[i][:, b, :], ident_b[:])
+            tb = new_bank("tb1", [P, P], BF16)
+            nc.tensor.transpose(tb[:], b2d[:], ident_b[:])
 
-        def table_out(i):
-            nc.scalar.copy(out=(ct, snt, b_pp, bv_bc)[i][:], in_=pst[("tb", i)][:])
+        def table_out():
+            nc.scalar.copy(out=cs[:], in_=bks["tb0"][:])
+            nc.scalar.copy(out=b_pp[:], in_=bks["tb1"][:])
 
-        def x_turn(ip, g):
-            xt = psp.tile([P, 2, 2, P], F32, name="xt%d%d" % (ip, g), tag="ps")
-            pst[("xt", ip, g)] = xt
-            for a in range(2):
-                words = x_sb[:, 2 * ip + a, :].bitcast(F32)
+        def load_vbias():
+            nc.sync.dma_start(out=bv_bc[:], in_=qkv_bias[5 * GW:6 * GW].partition_broadcast(P))
+
+        def x_turn(ip, a):
+            words = x_sb[:, 2 * ip + a, :].bitcast(F32)
+            for g in range(NG):
+                if a == 0:
+                    new_bank("xt%d%d" % (g, ip), [P, 2, 2, P], F32)
+                xt = bks["xt%d%d" % (g, ip)]
                 for u in range(2):
-                    nc.tensor.transpose(xt[:, a, u, :], words[:, 256 * g + u:256 * (g + 1):2],
-                                        ident_f[:])
+                    nc.tensor.transpose(xt[:, a, u, :], words[:, 256 * g + u:256 * (g + 1):2], ident_f[:])
 
-        def x_out(ip, g, eng):
+        def x_out(g, ip, eng):
             if g // 2 not in gxs:
                 gx = outp.tile([P, 2, 4 * S_TOK], BF16, name="gx%d" % (g // 2), tag="o", align_bytes=64)
                 gxs[g // 2] = gx
             dst = gxs[g // 2][:, g % 2, :].bitcast(F32).rearrange("p (i r u) -> p i r u", i=4, u=2)
-            src = pst[("xt", ip, g)][:].rearrange("p a u r -> p a r u")
+            src = bks["xt%d%d" % (g, ip)][:].rearrange("p a u r -> p a r u")
             if eng == "V":
                 nc.vector.tensor_copy(out=dst[:, 2 * ip:2 * ip + 2, :, :], in_=src)
             else:
                 nc.scalar.copy(out=dst[:, 2 * ip:2 * ip + 2, :, :], in_=src)
 
-        def quant_x(g):
-            nc.vector.quantize_mx(out=xc[:, g, :].bitcast(E5X4), scales=xs[:, g, :],
-                                  in_=gxs[g // 2][:, g % 2, :])
+        def quant_x(g, ip):
+            nc.vector.quantize_mx(out=xc[:, g, ip * 256:(ip + 1) * 256].bitcast(E5X4),
+                                  scales=xs[:, g, ip * 256:(ip + 1) * 256],
+                                  in_=gxs[g // 2][:, g % 2, ip * 1024:(ip + 1) * 1024])
 
-        def group_tile(n, g, eng):
+        def unit_tile(n, g, pool):
             if (n, g) not in grs:
-                if eng == "S":
+                if pool == "S":
                     gr = grps.tile([P, 4 * GW], BF16, name="gr%d%d" % (n, g), tag="grs", align_bytes=64)
                     grs[(n, g)] = gr[:]
-                elif eng == "V":
+                elif pool == "V":
                     gr = grpv.tile([P, 4 * GW], BF16, name="gr%d%d" % (n, g), tag="grv", align_bytes=64)
                     grs[(n, g)] = gr[:]
                 else:
-                    pair = G_UNITS[n]
                     gr = grpg.tile([P, 2, 4 * GW], BF16, name="grg%d" % n, tag="grg", align_bytes=64)
-                    grs[(n, pair[0])] = gr[:, 0, :]
-                    grs[(n, pair[1])] = gr[:, 1, :]
+                    grs[(n, pool[0])] = gr[:, 0, :]
+                    grs[(n, pool[1])] = gr[:, 1, :]
             return grs[(n, g)]
 
-        def copy_unit(n, g, eng):
-            interleave(group_tile(n, g, eng), raws[n][:, g, :, :], eng)
-
-        def copy_half(n, g, h, eng):
-            gr = group_tile(n, g, "G")
-            interleave(gr[:, h * 2 * GW:(h + 1) * 2 * GW], raws[n][:, g, :, h * 256:(h + 1) * 256], eng)
-
-        def interleave(gr, raw, eng):
-            if PAT_B and eng != "G":
+        def copy(n, g, eng, pool=None, c0=0, c1=GW):
+            gr = unit_tile(n, g, pool or eng)[:, 4 * c0:4 * c1]
+            raw = raws[n][:, g, :, c0:c1]
+            if eng != "G":
                 dst = gr.rearrange("p (c i j) -> p c j i", i=4, j=4)
                 src = raw.rearrange("p j (c i) -> p c j i", i=4)
             else:
@@ -192,47 +171,44 @@ def tile_attentioncore_pa_kernel(tc, x, qkv_kernel, qkv_bias, cos_table, sin_tab
             else:
                 nc.gpsimd.tensor_scalar(out=dst, in0=src, scalar1=1.0, scalar2=0.0, op0=MULT, op1=ADD)
 
-        def quant_unit(n, g):
+        def quant(n, g):
             nc.vector.quantize_mx(out=wcs[n][:, g, :].bitcast(E5X4), scales=wss[n][:, g, :],
                                   in_=grs[(n, g)])
 
         def mx(m, g):
             if g == 0:
-                acc_new = accp.tile([P, S_TOK], F32, name="acc%d" % m, tag="acc")
-                accs[m] = acc_new
+                new_bank(m, [P, 1, S_TOK], F32)
+            acc = bks[m][:, 0, :]
             if m < 20:
                 n = m // 4
                 cols = slice((m % 4) * P, (m % 4 + 1) * P)
-                nc.tensor.matmul_mx(out=accs[m][:],
+                nc.tensor.matmul_mx(out=acc,
                                     lhsT=wcs[n][:, g, cols].bitcast(E5X4), lhsT_scale=wss[n][:, g, cols],
                                     rhs=xc[:, g, :].bitcast(E5X4), rhs_scale=xs[:, g, :],
                                     start=(g == 0), stop=(g == NG - 1))
             else:
                 cols = slice((m - 20) * P, (m - 19) * P)
-                nc.tensor.matmul_mx(out=accs[m][:],
+                nc.tensor.matmul_mx(out=acc,
                                     lhsT=xc[:, g, cols].bitcast(E5X4), lhsT_scale=xs[:, g, cols],
                                     rhs=wcs[5][:, g, :].bitcast(E5X4), rhs_scale=wss[5][:, g, :],
                                     start=(g == 0), stop=(g == NG - 1))
 
-        def rot_t(m):
-            t_t = tup.tile([P, S_TOK], F32, name="t%d" % m, tag="t")
-            tts[m] = t_t
-            nc.vector.scalar_tensor_tensor(out=t_t[:], in0=accs[m][:], scalar=b_pp[:, m:m + 1],
-                                           in1=ct[:], op0=ADD, op1=MULT)
+        def mx_tile(m):
+            for g in range(NG):
+                mx(m, g)
 
-        def rot_u(m):
-            u_t = tup.tile([P, S_TOK], F32, name="u%d" % m, tag="u")
-            uts[m] = u_t
-            nc.vector.scalar_tensor_tensor(out=u_t[:], in0=accs[m][:], scalar=b_pp[:, m:m + 1],
-                                           in1=snt[:], op0=ADD, op1=MULT)
+        def rot(m):
+            tu = tup.tile([P, 2, S_TOK], F32, name="tu%d" % m, tag="tu")
+            tus[m] = tu
+            nc.vector.scalar_tensor_tensor(out=tu[:], in0=bks[m][:].to_broadcast([P, 2, S_TOK]),
+                                           scalar=b_pp[:, m:m + 1], in1=cs[:], op0=ADD, op1=MULT)
 
         def back(m):
-            tr = psp.tile([P, 4, P], F32, name="tr%d" % m, tag="ps")
-            pst[("tr", m)] = tr
+            tr = bks[m][:, 0, :].rearrange("p (i c) -> p i c", i=4)
             for i in range(4):
-                nc.tensor.matmul(out=tr[:, i, :], lhsT=tts[m][:, i * P:(i + 1) * P], rhs=ident_f[:],
+                nc.tensor.matmul(out=tr[:, i, :], lhsT=tus[m][:, 0, i * P:(i + 1) * P], rhs=ident_f[:],
                                  is_transpose=True, start=True, stop=False)
-                nc.tensor.matmul(out=tr[:, i, :], lhsT=uts[m][:, i * P:(i + 1) * P], rhs=perm_f[:],
+                nc.tensor.matmul(out=tr[:, i, :], lhsT=tus[m][:, 1, i * P:(i + 1) * P], rhs=perm_f[:],
                                  is_transpose=True, start=False, stop=True)
 
         def leave(m):
@@ -240,7 +216,8 @@ def tile_attentioncore_pa_kernel(tc, x, qkv_kernel, qkv_bias, cos_table, sin_tab
             if n not in outs:
                 o_new = outp.tile([P, 4, GW], F32, name="o%d" % n, tag="o", align_bytes=64)
                 outs[n] = o_new
-            nc.scalar.copy(out=outs[n][:, :, (m % 4) * P:(m % 4 + 1) * P], in_=pst[("tr", m)][:])
+            nc.scalar.copy(out=outs[n][:, :, (m % 4) * P:(m % 4 + 1) * P],
+                           in_=bks[m][:, 0, :].rearrange("p (i c) -> p i c", i=4))
 
         def store_q(n):
             nc.scalar.dma_start(out=q3[:, :, n * GW:(n + 1) * GW], in_=outs[n][:])
@@ -252,313 +229,91 @@ def tile_attentioncore_pa_kernel(tc, x, qkv_kernel, qkv_bias, cos_table, sin_tab
         def v_out(i):
             vo = vop.tile([P, GW], F32, name="vo%d" % i, tag="vo")
             vos[i] = vo
-            nc.vector.tensor_tensor(out=vo[:], in0=accs[20 + i][:], in1=bv_bc[:], op=ADD)
+            nc.vector.tensor_tensor(out=vo[:], in0=bks[20 + i][:, 0, :], in1=bv_bc[:], op=ADD)
+
+        def v_out_sg(i):
+            va = vop.tile([P, GW], F32, name="va%d" % i, tag="va")
+            vo = vop.tile([P, GW], F32, name="vo%d" % i, tag="vo")
+            vos[i] = vo
+            nc.scalar.copy(out=va[:], in_=bks[20 + i][:, 0, :])
+            nc.gpsimd.tensor_tensor(out=vo[:], in0=va[:], in1=bv_bc[:], op=ADD)
 
         def v_store(i):
             nc.sync.dma_start(out=v2[i * P:(i + 1) * P, :], in_=vos[i][:])
 
+
+        VC0 = 256
+        VC1 = 224
         nc.gpsimd.memset(b2d[:], 0.0)
         load_tabs()
-        load_bias()
         load_w(0, 0)
-        load_w(0, 1)
-        load_x(0)
-        load_x(1)
-        load_x(2)
-        load_x(3)
-        load_w(0, 2)
-        load_w(0, 3)
-        load_w(1, 0)
-        load_w(1, 1)
-        load_w(1, 2)
-        load_w(1, 3)
-        load_w(2, 0)
-        load_w(2, 1)
-        load_w(2, 2)
-        load_w(2, 3)
-        load_w(3, 0)
-        load_w(3, 1)
-        load_w(3, 2)
-        load_w(3, 3)
-        load_w(4, 0)
-        load_w(4, 1)
-        load_w(4, 2)
-        load_w(4, 3)
-        load_w(5, 0)
-        load_w(5, 1)
-        load_w(5, 2)
-        load_w(5, 3)
-        make_ident()
+        for i in range(4):
+            load_x(i)
+        for g in range(1, NG):
+            load_w(0, g)
+        for n in range(1, NGRP):
+            for g in range(NG):
+                load_w(n, g)
+        load_vbias()
+        make_identity(nc, ident_f[:])
         consts_v()
+        copy(0, 0, "V")
         tables_v()
-        table_pe(0)
-        table_out(0)
-        table_pe(1)
-        table_out(1)
-        table_pe(2)
-        table_out(2)
-        table_pe(3)
-        table_out(3)
-        copy_unit(0, 0, "G")
-        copy_unit(0, 1, "G")
-        quant_unit(0, 0)
-        quant_unit(0, 1)
+        quant(0, 0)
         x_turn(0, 0)
-        x_out(0, 0, "S")
         x_turn(0, 1)
-        x_out(0, 1, "S")
-        x_turn(0, 2)
-        x_out(0, 2, "S")
-        x_turn(0, 3)
-        x_out(0, 3, "S")
+        for g in range(NG):
+            x_out(g, 0, "S")
+            quant_x(g, 0)
         x_turn(1, 0)
-        x_out(1, 0, "S")
         x_turn(1, 1)
-        x_out(1, 1, "S")
-        x_turn(1, 2)
-        x_out(1, 2, "S")
-        x_turn(1, 3)
-        x_out(1, 3, "S")
-        copy_unit(0, 2, "S")
-        quant_x(0)
-        quant_x(1)
-        mx(0, 0)
-        mx(1, 0)
-        mx(2, 0)
-        mx(3, 0)
-        quant_x(2)
-        mx(0, 1)
-        mx(1, 1)
-        mx(2, 1)
-        mx(3, 1)
-        quant_x(3)
-        copy_unit(0, 3, "V")
-        quant_unit(0, 2)
-        mx(0, 2)
-        mx(1, 2)
-        mx(2, 2)
-        mx(3, 2)
-        quant_unit(0, 3)
-        mx(0, 3)
-        mx(1, 3)
-        mx(2, 3)
-        mx(3, 3)
-        copy_unit(1, 0, "S")
-        copy_unit(1, 2, "S")
-        copy_unit(1, 1, "G")
-        copy_half(1, 3, 0, "G")
-        rot_t(0)
-        rot_u(0)
-        rot_t(1)
-        rot_u(1)
-        copy_half(1, 3, 1, "V")
-        quant_unit(1, 0)
-        quant_unit(1, 2)
-        quant_unit(1, 1)
-        quant_unit(1, 3)
-        copy_unit(2, 1, "G")
-        copy_half(2, 3, 0, "G")
-        back(0)
-        back(1)
-        copy_unit(2, 0, "S")
-        leave(0)
-        leave(1)
-        mx(4, 0)
-        mx(5, 0)
-        mx(4, 1)
-        mx(5, 1)
-        mx(4, 2)
-        mx(5, 2)
-        mx(4, 3)
-        mx(5, 3)
-        rot_t(2)
-        rot_u(2)
-        rot_t(3)
-        rot_u(3)
-        back(2)
-        back(3)
-        copy_unit(2, 2, "S")
-        leave(2)
-        leave(3)
-        store_q(0)
-        mx(6, 0)
-        mx(6, 1)
-        mx(6, 2)
-        mx(6, 3)
-        mx(7, 0)
-        mx(7, 1)
-        mx(7, 2)
-        mx(7, 3)
-        rot_t(4)
-        rot_u(4)
-        rot_t(5)
-        rot_u(5)
-        copy_half(2, 3, 1, "V")
-        quant_unit(2, 0)
-        quant_unit(2, 2)
-        quant_unit(2, 1)
-        quant_unit(2, 3)
-        copy_unit(3, 1, "G")
-        copy_half(3, 3, 0, "G")
-        back(4)
-        back(5)
-        copy_unit(3, 0, "S")
-        leave(4)
-        leave(5)
-        mx(8, 0)
-        mx(8, 1)
-        mx(8, 2)
-        mx(8, 3)
-        mx(9, 0)
-        mx(9, 1)
-        mx(9, 2)
-        mx(9, 3)
-        rot_t(6)
-        rot_u(6)
-        rot_t(7)
-        rot_u(7)
-        back(6)
-        back(7)
-        copy_unit(3, 2, "S")
-        leave(6)
-        leave(7)
-        store_q(1)
-        mx(10, 0)
-        mx(10, 1)
-        mx(10, 2)
-        mx(10, 3)
-        mx(11, 0)
-        mx(11, 1)
-        mx(11, 2)
-        mx(11, 3)
-        rot_t(8)
-        rot_u(8)
-        rot_t(9)
-        rot_u(9)
-        copy_half(3, 3, 1, "V")
-        quant_unit(3, 0)
-        quant_unit(3, 2)
-        quant_unit(3, 1)
-        quant_unit(3, 3)
-        copy_unit(4, 1, "G")
-        copy_half(4, 3, 0, "G")
-        back(8)
-        back(9)
-        copy_unit(4, 0, "S")
-        leave(8)
-        leave(9)
-        mx(12, 0)
-        mx(12, 1)
-        mx(12, 2)
-        mx(12, 3)
-        mx(13, 0)
-        mx(13, 1)
-        mx(13, 2)
-        mx(13, 3)
-        rot_t(10)
-        rot_u(10)
-        rot_t(11)
-        rot_u(11)
-        back(10)
-        back(11)
-        copy_unit(4, 2, "S")
-        leave(10)
-        leave(11)
-        store_q(2)
-        mx(14, 0)
-        mx(14, 1)
-        mx(14, 2)
-        mx(14, 3)
-        mx(15, 0)
-        mx(15, 1)
-        mx(15, 2)
-        mx(15, 3)
-        rot_t(12)
-        rot_u(12)
-        rot_t(13)
-        rot_u(13)
-        copy_half(4, 3, 1, "V")
-        quant_unit(4, 0)
-        quant_unit(4, 2)
-        quant_unit(4, 1)
-        quant_unit(4, 3)
-        copy_unit(5, 1, "G")
-        copy_half(5, 3, 0, "G")
-        back(12)
-        back(13)
-        copy_unit(5, 0, "S")
-        leave(12)
-        leave(13)
-        mx(16, 0)
-        mx(16, 1)
-        mx(16, 2)
-        mx(16, 3)
-        mx(17, 0)
-        mx(17, 1)
-        mx(17, 2)
-        mx(17, 3)
-        rot_t(14)
-        rot_u(14)
-        rot_t(15)
-        rot_u(15)
-        back(14)
-        back(15)
-        copy_unit(5, 2, "S")
-        leave(14)
-        leave(15)
-        store_q(3)
-        mx(18, 0)
-        mx(18, 1)
-        mx(18, 2)
-        mx(18, 3)
-        mx(19, 0)
-        mx(19, 1)
-        mx(19, 2)
-        mx(19, 3)
-        rot_t(16)
-        rot_u(16)
-        rot_t(17)
-        rot_u(17)
-        copy_half(5, 3, 1, "V")
-        quant_unit(5, 0)
-        quant_unit(5, 2)
-        quant_unit(5, 1)
-        quant_unit(5, 3)
-        back(16)
-        back(17)
-        leave(16)
-        leave(17)
-        store_k(0)
-        mx(20, 0)
-        mx(20, 1)
-        mx(20, 2)
-        mx(20, 3)
-        mx(21, 0)
-        mx(21, 1)
-        mx(21, 2)
-        mx(21, 3)
-        rot_t(18)
-        rot_u(18)
-        rot_t(19)
-        rot_u(19)
-        back(18)
-        back(19)
-        leave(18)
-        leave(19)
-        store_k(1)
-        mx(22, 0)
-        mx(22, 1)
-        mx(22, 2)
-        mx(22, 3)
-        mx(23, 0)
-        mx(23, 1)
-        mx(23, 2)
-        mx(23, 3)
-        v_out(0)
-        v_store(0)
-        v_out(1)
-        v_store(1)
-        v_out(2)
-        v_store(2)
-        v_out(3)
-        v_store(3)
+        for g in range(NG):
+            x_out(g, 1, "S" if g % 2 == 0 else "V")
+        for g in range(NG):
+            quant_x(g, 1)
+        for m in range(4):
+            mx(m, 0)
+        table_pe()
+
+        for g in range(1, NG):
+            copy(0, g, "V", "S", 0, VC0)
+            copy(0, g, "S", "S", VC0, GW)
+            quant(0, g)
+            for m in range(4):
+                mx(m, g)
+        table_out()
+        for g in range(NG):
+            pool = "S" if g % 2 == 0 else (1, 3)
+            copy(1, g, "V", pool, 0, VC1)
+            copy(1, g, "S", pool, VC1, GW)
+            quant(1, g)
+
+        for n in range(1, NGRP):
+            for m in range(4 * n - 4, 4 * n):
+                rot(m)
+            if n + 1 < NGRP:
+                copy(n + 1, 1, "G", (1, 3))
+                copy(n + 1, 3, "G", (1, 3), 0, 256)
+                copy(n + 1, 0, "S")
+                copy(n + 1, 2, "S")
+            if n < 5:
+                for g in range(NG):
+                    for m in range(4 * n, 4 * n + 4):
+                        mx(m, g)
+                for m in range(4 * n - 4, 4 * n):
+                    back(m)
+                    leave(m)
+                store_q(n - 1)
+                copy(n + 1, 3, "V", (1, 3), 256, GW)
+                for g in range(NG):
+                    quant(n + 1, g)
+            else:
+                for i in range(4):
+                    mx_tile(20 + i)
+                    v_out_sg(i)
+                    v_store(i)
+                for m in range(16, 20):
+                    back(m)
+                    leave(m)
+                    if m % 2 == 1:
+                        store_k((m - 16) // 2)

@@ -45,7 +45,7 @@ def tile_attentioncore_pa_kernel(tc, x, qkv_kernel, qkv_bias, cos_table, sin_tab
         e_s = const.tile([P, 4, P], BF16, name="e_s", tag="e_s")
         cs = const.tile([P, 2, S_TOK], BF16, name="cs", tag="cs")
         b_pp = const.tile([P, P], F32, name="b_pp", tag="b_pp")
-        bv_bc = const.tile([P, GW], BF16, name="bv_bc", tag="bv_bc")
+        bv_bc = const.tile([P, GW], F32, name="bv_bc", tag="bv_bc")
         xc = codes.tile([P, NG, S_TOK], U32, name="xc", tag="xc", align_bytes=64)
         xs = codes.tile([P, NG, S_TOK], U8, name="xs", tag="xs", align_bytes=64)
         wcs = []
@@ -108,13 +108,16 @@ def tile_attentioncore_pa_kernel(tc, x, qkv_kernel, qkv_bias, cos_table, sin_tab
                     nc.tensor.transpose(tb[:, i, b * P:(b + 1) * P], (e_c, e_s)[i][:, b, :], ident_b[:])
             tb = new_bank("tb1", [P, P], BF16)
             nc.tensor.transpose(tb[:], b2d[:], ident_b[:])
+            tb = new_bank("tb2", [P, GW], F32)
+            for r in range(4):
+                nc.tensor.matmul(out=tb[:, r * P:(r + 1) * P],
+                                 lhsT=ident_b[:, 20 + r:21 + r].to_broadcast([P, P]),
+                                 rhs=b2d[:], start=True, stop=True)
 
         def table_out():
             nc.scalar.copy(out=cs[:], in_=bks["tb0"][:])
             nc.scalar.copy(out=b_pp[:], in_=bks["tb1"][:])
-
-        def load_vbias():
-            nc.sync.dma_start(out=bv_bc[:], in_=qkv_bias[5 * GW:6 * GW].partition_broadcast(P))
+            nc.scalar.copy(out=bv_bc[:], in_=bks["tb2"][:])
 
         def x_turn(ip, a):
             words = x_sb[:, 2 * ip + a, :].bitcast(F32)
@@ -212,19 +215,20 @@ def tile_attentioncore_pa_kernel(tc, x, qkv_kernel, qkv_bias, cos_table, sin_tab
                                  is_transpose=True, start=False, stop=True)
 
         def leave(m):
-            n = m // 4
-            if n not in outs:
-                o_new = outp.tile([P, 4, GW], F32, name="o%d" % n, tag="o", align_bytes=64)
-                outs[n] = o_new
-            nc.scalar.copy(out=outs[n][:, :, (m % 4) * P:(m % 4 + 1) * P],
+            key = m // 4 if m < 16 else 4 + (m - 16) // 2
+            width = GW if m < 16 else 2 * P
+            if key not in outs:
+                o_new = outp.tile([P, 4, width], F32, name="o%d" % key, tag="o", align_bytes=64)
+                outs[key] = o_new
+            col = (m % 4) * P if m < 16 else (m % 2) * P
+            nc.scalar.copy(out=outs[key][:, :, col:col + P],
                            in_=bks[m][:, 0, :].rearrange("p (i c) -> p i c", i=4))
 
         def store_q(n):
             nc.scalar.dma_start(out=q3[:, :, n * GW:(n + 1) * GW], in_=outs[n][:])
 
         def store_k(h):
-            half = slice(h * 2 * P, (h + 1) * 2 * P)
-            nc.scalar.dma_start(out=k3[:, :, half], in_=outs[4][:, :, half])
+            nc.scalar.dma_start(out=k3[:, :, h * 2 * P:(h + 1) * 2 * P], in_=outs[4 + h][:])
 
         def v_out(i):
             vo = vop.tile([P, GW], F32, name="vo%d" % i, tag="vo")
@@ -241,52 +245,87 @@ def tile_attentioncore_pa_kernel(tc, x, qkv_kernel, qkv_bias, cos_table, sin_tab
         def v_store(i):
             nc.sync.dma_start(out=v2[i * P:(i + 1) * P, :], in_=vos[i][:])
 
-
-        VC0 = 256
-        VC1 = 224
         nc.gpsimd.memset(b2d[:], 0.0)
         load_tabs()
         load_w(0, 0)
-        for i in range(4):
-            load_x(i)
-        for g in range(1, NG):
-            load_w(0, g)
-        for n in range(1, NGRP):
+        load_x(0)
+        load_x(1)
+        load_x(2)
+        load_x(3)
+        load_w(0, 1)
+        load_w(0, 2)
+        load_w(0, 3)
+        load_w(1, 0)
+        load_w(1, 1)
+        load_w(1, 2)
+        load_w(1, 3)
+        for n in range(2, NGRP):
             for g in range(NG):
                 load_w(n, g)
-        load_vbias()
         make_identity(nc, ident_f[:])
         consts_v()
-        copy(0, 0, "V")
+        copy(0, 0, "V", "S", 0, 512)
         tables_v()
         quant(0, 0)
         x_turn(0, 0)
         x_turn(0, 1)
-        for g in range(NG):
-            x_out(g, 0, "S")
-            quant_x(g, 0)
+        x_out(0, 0, "S")
+        x_out(1, 0, "S")
+        x_out(2, 0, "S")
+        x_out(3, 0, "S")
+        quant_x(0, 0)
+        quant_x(1, 0)
+        quant_x(2, 0)
+        quant_x(3, 0)
         x_turn(1, 0)
         x_turn(1, 1)
-        for g in range(NG):
-            x_out(g, 1, "S" if g % 2 == 0 else "V")
-        for g in range(NG):
-            quant_x(g, 1)
-        for m in range(4):
-            mx(m, 0)
+        x_out(0, 1, "S")
+        x_out(1, 1, "V")
+        x_out(2, 1, "S")
+        x_out(3, 1, "V")
+        quant_x(0, 1)
+        quant_x(1, 1)
+        quant_x(2, 1)
+        quant_x(3, 1)
         table_pe()
-
-        for g in range(1, NG):
-            copy(0, g, "V", "S", 0, VC0)
-            copy(0, g, "S", "S", VC0, GW)
-            quant(0, g)
-            for m in range(4):
-                mx(m, g)
+        for m in range(0, 4):
+            mx(m, 0)
+        copy(0, 1, "V", "S", 0, 256)
+        copy(0, 1, "S", "S", 256, GW)
+        copy(0, 2, "V", "S", 0, 256)
+        copy(0, 2, "S", "S", 256, GW)
+        quant(0, 1)
+        for m in range(0, 4):
+            mx(m, 1)
+        copy(0, 3, "V", "S", 0, 256)
+        copy(0, 3, "S", "S", 256, GW)
+        quant(0, 2)
+        for m in range(0, 4):
+            mx(m, 2)
+        copy(1, 0, "V", "S", 0, 224)
+        copy(1, 0, "S", "S", 224, GW)
+        quant(0, 3)
+        for m in range(0, 4):
+            mx(m, 3)
+        copy(1, 1, "V", (1, 3), 0, 224)
+        copy(1, 1, "S", (1, 3), 224, GW)
+        quant(1, 0)
+        for m in range(4, 8):
+            mx(m, 0)
+        copy(1, 2, "V", "S", 0, 224)
+        copy(1, 2, "S", "S", 224, GW)
+        quant(1, 1)
+        for m in range(4, 8):
+            mx(m, 1)
+        copy(1, 3, "V", (1, 3), 0, 224)
+        copy(1, 3, "S", (1, 3), 224, GW)
+        quant(1, 2)
+        for m in range(4, 8):
+            mx(m, 2)
+        quant(1, 3)
+        for m in range(4, 8):
+            mx(m, 3)
         table_out()
-        for g in range(NG):
-            pool = "S" if g % 2 == 0 else (1, 3)
-            copy(1, g, "V", pool, 0, VC1)
-            copy(1, g, "S", pool, VC1, GW)
-            quant(1, g)
 
         for n in range(1, NGRP):
             for m in range(4 * n - 4, 4 * n):
@@ -297,23 +336,28 @@ def tile_attentioncore_pa_kernel(tc, x, qkv_kernel, qkv_bias, cos_table, sin_tab
                 copy(n + 1, 0, "S")
                 copy(n + 1, 2, "S")
             if n < 5:
-                for g in range(NG):
-                    for m in range(4 * n, 4 * n + 4):
-                        mx(m, g)
+                if n > 1 or False:
+                    for g in range(NG):
+                        for m in range(4 * n, 4 * n + 4):
+                            mx(m, g)
                 for m in range(4 * n - 4, 4 * n):
                     back(m)
                     leave(m)
                 store_q(n - 1)
                 copy(n + 1, 3, "V", (1, 3), 256, GW)
-                for g in range(NG):
+                for g in (0, 1, 2, 3):
                     quant(n + 1, g)
             else:
                 for i in range(4):
                     mx_tile(20 + i)
-                    v_out_sg(i)
-                    v_store(i)
+                    if i < 2:
+                        v_out_sg(i)
+                        v_store(i)
                 for m in range(16, 20):
                     back(m)
                     leave(m)
                     if m % 2 == 1:
                         store_k((m - 16) // 2)
+                for i in range(2, 4):
+                    v_out(i)
+                    v_store(i)

@@ -108,16 +108,18 @@ def tile_attentioncore_pa_kernel(tc, x, qkv_kernel, qkv_bias, cos_table, sin_tab
                     nc.tensor.transpose(tb[:, i, b * P:(b + 1) * P], (e_c, e_s)[i][:, b, :], ident_b[:])
             tb = new_bank("tb1", [P, P], BF16)
             nc.tensor.transpose(tb[:], b2d[:], ident_b[:])
+
+        def table_out():
+            nc.scalar.copy(out=cs[:], in_=bks["tb0"][:])
+            nc.scalar.copy(out=b_pp[:], in_=bks["tb1"][:])
+
+        def vbias():
             tb = new_bank("tb2", [P, GW], F32)
             for r in range(4):
                 nc.tensor.matmul(out=tb[:, r * P:(r + 1) * P],
                                  lhsT=ident_b[:, 20 + r:21 + r].to_broadcast([P, P]),
                                  rhs=b2d[:], start=True, stop=True)
-
-        def table_out():
-            nc.scalar.copy(out=cs[:], in_=bks["tb0"][:])
-            nc.scalar.copy(out=b_pp[:], in_=bks["tb1"][:])
-            nc.scalar.copy(out=bv_bc[:], in_=bks["tb2"][:])
+            nc.scalar.copy(out=bv_bc[:], in_=tb[:])
 
         def x_turn(ip, a):
             words = x_sb[:, 2 * ip + a, :].bitcast(F32)
@@ -279,6 +281,7 @@ def tile_attentioncore_pa_kernel(tc, x, qkv_kernel, qkv_bias, cos_table, sin_tab
         quant_x(3, 0)
         x_turn(1, 0)
         x_turn(1, 1)
+        table_pe()
         x_out(0, 1, "S")
         x_out(1, 1, "V")
         x_out(2, 1, "S")
@@ -287,11 +290,11 @@ def tile_attentioncore_pa_kernel(tc, x, qkv_kernel, qkv_bias, cos_table, sin_tab
         quant_x(1, 1)
         quant_x(2, 1)
         quant_x(3, 1)
-        table_pe()
         for m in range(0, 4):
             mx(m, 0)
         copy(0, 1, "V", "S", 0, 256)
         copy(0, 1, "S", "S", 256, GW)
+        table_out()
         copy(0, 2, "V", "S", 0, 256)
         copy(0, 2, "S", "S", 256, GW)
         quant(0, 1)
@@ -325,7 +328,6 @@ def tile_attentioncore_pa_kernel(tc, x, qkv_kernel, qkv_bias, cos_table, sin_tab
         quant(1, 3)
         for m in range(4, 8):
             mx(m, 3)
-        table_out()
 
         for n in range(1, NGRP):
             for m in range(4 * n - 4, 4 * n):
@@ -344,6 +346,8 @@ def tile_attentioncore_pa_kernel(tc, x, qkv_kernel, qkv_bias, cos_table, sin_tab
                     back(m)
                     leave(m)
                 store_q(n - 1)
+                if n == 4:
+                    vbias()
                 copy(n + 1, 3, "V", (1, 3), 256, GW)
                 for g in (0, 1, 2, 3):
                     quant(n + 1, g)

@@ -29,7 +29,7 @@ def tile_attentioncore_pa_kernel(tc, x, qkv_kernel, qkv_bias, cos_table, sin_tab
         grps = ctx.enter_context(tc.tile_pool(name="grps", bufs=4))
         grpv = ctx.enter_context(tc.tile_pool(name="grpv", bufs=1))
         grpg = ctx.enter_context(tc.tile_pool(name="grpg", bufs=1))
-        vop = ctx.enter_context(tc.tile_pool(name="vop", bufs=2))
+        vop = ctx.enter_context(tc.tile_pool(name="vop", bufs=4))
         codes = ctx.enter_context(tc.tile_pool(name="codes", bufs=1))
         tup = ctx.enter_context(tc.tile_pool(name="tup", bufs=4))
         outp = ctx.enter_context(tc.tile_pool(name="outp", bufs=2))
@@ -121,30 +121,29 @@ def tile_attentioncore_pa_kernel(tc, x, qkv_kernel, qkv_bias, cos_table, sin_tab
                                  rhs=b2d[:], start=True, stop=True)
             nc.scalar.copy(out=bv_bc[:], in_=tb[:])
 
-        def x_turn(ip, a):
-            words = x_sb[:, 2 * ip + a, :].bitcast(F32)
-            for g in range(NG):
-                if a == 0:
-                    new_bank("xt%d%d" % (g, ip), [P, 2, 2, P], F32)
-                xt = bks["xt%d%d" % (g, ip)]
-                for u in range(2):
-                    nc.tensor.transpose(xt[:, a, u, :], words[:, 256 * g + u:256 * (g + 1):2], ident_f[:])
+        def x_turn(i):
+            words = x_sb[:, i, :].bitcast(F32)
+            for gp in range(2):
+                xt = new_bank("xt%d%d" % (i, gp), [P, 2, 2, P], F32)
+                for a in range(2):
+                    g = 2 * gp + a
+                    for u in range(2):
+                        nc.tensor.transpose(xt[:, a, u, :], words[:, 256 * g + u:256 * (g + 1):2], ident_f[:])
 
-        def x_out(g, ip, eng):
-            if g // 2 not in gxs:
-                gx = outp.tile([P, 2, 4 * S_TOK], BF16, name="gx%d" % (g // 2), tag="o", align_bytes=64)
-                gxs[g // 2] = gx
-            dst = gxs[g // 2][:, g % 2, :].bitcast(F32).rearrange("p (i r u) -> p i r u", i=4, u=2)
-            src = bks["xt%d%d" % (g, ip)][:].rearrange("p a u r -> p a r u")
+        def x_out(i, gp, eng):
+            if i // 2 not in gxs:
+                gx = outp.tile([P, 2, NG, GW], BF16, name="gx%d" % (i // 2), tag="o", align_bytes=64)
+                gxs[i // 2] = gx
+            dst = gxs[i // 2][:, i % 2, 2 * gp:2 * gp + 2, :].bitcast(F32).rearrange("p g (r u) -> p g r u", u=2)
+            src = bks["xt%d%d" % (i, gp)][:].rearrange("p g u r -> p g r u")
             if eng == "V":
-                nc.vector.tensor_copy(out=dst[:, 2 * ip:2 * ip + 2, :, :], in_=src)
+                nc.vector.tensor_copy(out=dst, in_=src)
             else:
-                nc.scalar.copy(out=dst[:, 2 * ip:2 * ip + 2, :, :], in_=src)
+                nc.scalar.copy(out=dst, in_=src)
 
-        def quant_x(g, ip):
-            nc.vector.quantize_mx(out=xc[:, g, ip * 256:(ip + 1) * 256].bitcast(E5X4),
-                                  scales=xs[:, g, ip * 256:(ip + 1) * 256],
-                                  in_=gxs[g // 2][:, g % 2, ip * 1024:(ip + 1) * 1024])
+        def quant_x(g, i):
+            nc.vector.quantize_mx(out=xc[:, g, i * P:(i + 1) * P].bitcast(E5X4), scales=xs[:, g, i * P:(i + 1) * P],
+                                  in_=gxs[i // 2][:, i % 2, g, :])
 
         def unit_tile(n, g, pool):
             if (n, g) not in grs:
@@ -269,29 +268,37 @@ def tile_attentioncore_pa_kernel(tc, x, qkv_kernel, qkv_bias, cos_table, sin_tab
         copy(0, 0, "V", "S", 0, 512)
         tables_v()
         quant(0, 0)
-        x_turn(0, 0)
-        x_turn(0, 1)
+        x_turn(0)
         x_out(0, 0, "S")
-        x_out(1, 0, "S")
-        x_out(2, 0, "S")
-        x_out(3, 0, "S")
+        x_out(0, 1, "S")
         quant_x(0, 0)
         quant_x(1, 0)
         quant_x(2, 0)
         quant_x(3, 0)
-        x_turn(1, 0)
-        x_turn(1, 1)
-        table_pe()
-        x_out(0, 1, "S")
-        x_out(1, 1, "V")
-        x_out(2, 1, "S")
-        x_out(3, 1, "V")
+        x_turn(1)
+        x_out(1, 0, "S")
+        x_out(1, 1, "S")
         quant_x(0, 1)
         quant_x(1, 1)
         quant_x(2, 1)
         quant_x(3, 1)
+        x_turn(2)
+        x_out(2, 0, "S")
+        x_out(2, 1, "S")
+        quant_x(0, 2)
+        quant_x(1, 2)
+        quant_x(2, 2)
+        quant_x(3, 2)
+        x_turn(3)
+        table_pe()
+        x_out(3, 0, "S")
+        x_out(3, 1, "V")
+        quant_x(0, 3)
         for m in range(0, 4):
             mx(m, 0)
+        quant_x(1, 3)
+        quant_x(2, 3)
+        quant_x(3, 3)
         copy(0, 1, "V", "S", 0, 256)
         copy(0, 1, "S", "S", 256, GW)
         table_out()
@@ -334,7 +341,7 @@ def tile_attentioncore_pa_kernel(tc, x, qkv_kernel, qkv_bias, cos_table, sin_tab
                 rot(m)
             if n + 1 < NGRP:
                 copy(n + 1, 1, "G", (1, 3))
-                copy(n + 1, 3, "G", (1, 3), 0, 256)
+                copy(n + 1, 3, "G", (1, 3), 0, 320)
                 copy(n + 1, 0, "S")
                 copy(n + 1, 2, "S")
             if n < 5:
@@ -348,7 +355,7 @@ def tile_attentioncore_pa_kernel(tc, x, qkv_kernel, qkv_bias, cos_table, sin_tab
                 store_q(n - 1)
                 if n == 4:
                     vbias()
-                copy(n + 1, 3, "V", (1, 3), 256, GW)
+                copy(n + 1, 3, "V", (1, 3), 320, GW)
                 for g in (0, 1, 2, 3):
                     quant(n + 1, g)
             else:

@@ -32,12 +32,14 @@ def tile_attentioncore_pa_kernel(tc, x, qkv_kernel, qkv_bias, cos_table, sin_tab
         vop = ctx.enter_context(tc.tile_pool(name="vop", bufs=4))
         codes = ctx.enter_context(tc.tile_pool(name="codes", bufs=1))
         tup = ctx.enter_context(tc.tile_pool(name="tup", bufs=4))
-        outp = ctx.enter_context(tc.tile_pool(name="outp", bufs=2))
+        outp = ctx.enter_context(tc.tile_pool(name="outp", bufs=4))
         bank = ctx.enter_context(tc.psum_pool(name="bank", bufs=8))
         ctx.enter_context(tc.manual_schedule())
 
         b2d = const.tile([P, P], BF16, name="b2d", tag="b2d")
-        x_sb = const.tile([P, 4, H], BF16, name="x_sb", tag="x_sb")
+        xs_a = outp.tile([P, 2, H], BF16, name="xs_a", tag="o", align_bytes=64)
+        xs_b = outp.tile([P, 2, H], BF16, name="xs_b", tag="o", align_bytes=64)
+        x_sbs = (xs_a, xs_b)
         ident_f = const.tile([P, P], F32, name="ident_f", tag="ident_f")
         ident_b = const.tile([P, P], BF16, name="ident_b", tag="ident_b")
         perm_f = const.tile([P, P], F32, name="perm_f", tag="perm_f")
@@ -72,7 +74,7 @@ def tile_attentioncore_pa_kernel(tc, x, qkv_kernel, qkv_bias, cos_table, sin_tab
             nc.scalar.dma_start(out=b2d[0:24, :], in_=qkv_bias.rearrange("(r c) -> r c", c=P))
 
         def load_x(i):
-            nc.sync.dma_start(out=x_sb[:, i, :], in_=x[i * P:(i + 1) * P, :])
+            nc.sync.dma_start(out=x_sbs[i // 2][:, i % 2, :], in_=x[i * P:(i + 1) * P, :])
 
         def load_w(n, g):
             if n not in raws:
@@ -122,7 +124,7 @@ def tile_attentioncore_pa_kernel(tc, x, qkv_kernel, qkv_bias, cos_table, sin_tab
             nc.scalar.copy(out=bv_bc[:], in_=tb[:])
 
         def x_turn(i):
-            words = x_sb[:, i, :].bitcast(F32)
+            words = x_sbs[i // 2][:, i % 2, :].bitcast(F32)
             for gp in range(2):
                 xt = new_bank("xt%d%d" % (i, gp), [P, 2, 2, P], F32)
                 for a in range(2):
@@ -226,7 +228,7 @@ def tile_attentioncore_pa_kernel(tc, x, qkv_kernel, qkv_bias, cos_table, sin_tab
                            in_=bks[m][:, 0, :].rearrange("p (i c) -> p i c", i=4))
 
         def store_q(n):
-            nc.scalar.dma_start(out=q3[:, :, n * GW:(n + 1) * GW], in_=outs[n][:])
+            nc.sync.dma_start(out=q3[:, :, n * GW:(n + 1) * GW], in_=outs[n][:])
 
         def store_k(h):
             nc.scalar.dma_start(out=k3[:, :, h * 2 * P:(h + 1) * 2 * P], in_=outs[4 + h][:])

@@ -346,6 +346,7 @@ def tile_attentioncore_pa_kernel(tc, x, qkv_kernel, qkv_bias, cos_table, sin_tab
                 copy(n + 1, 3, "G", (1, 3), 0, 320)
                 copy(n + 1, 0, "S")
                 copy(n + 1, 2, "S")
+                copy(n + 1, 3, "S", (1, 3), 320, GW)
             if n < 5:
                 if n > 1 or False:
                     for g in range(NG):
@@ -357,7 +358,6 @@ def tile_attentioncore_pa_kernel(tc, x, qkv_kernel, qkv_bias, cos_table, sin_tab
                 store_q(n - 1)
                 if n == 4:
                     vbias()
-                copy(n + 1, 3, "V", (1, 3), 320, GW)
                 for g in (0, 1, 2, 3):
                     quant(n + 1, g)
             else:

@@ -47,7 +47,7 @@ def tile_attentioncore_pa_kernel(tc, x, qkv_kernel, qkv_bias, cos_table, sin_tab
         e_s = const.tile([P, 4, P], BF16, name="e_s", tag="e_s")
         cs = const.tile([P, 2, S_TOK], BF16, name="cs", tag="cs")
         b_pp = const.tile([P, P], F32, name="b_pp", tag="b_pp")
-        bv_bc = const.tile([P, GW], F32, name="bv_bc", tag="bv_bc")
+        bv_bc = const.tile([P, GW], BF16, name="bv_bc", tag="bv_bc")
         xc = codes.tile([P, NG, S_TOK], U32, name="xc", tag="xc", align_bytes=64)
         xs = codes.tile([P, NG, S_TOK], U8, name="xs", tag="xs", align_bytes=64)
         wcs = []
@@ -116,12 +116,7 @@ def tile_attentioncore_pa_kernel(tc, x, qkv_kernel, qkv_bias, cos_table, sin_tab
             nc.scalar.copy(out=b_pp[:], in_=bks["tb1"][:])
 
         def vbias():
-            tb = new_bank("tb2", [P, GW], F32)
-            for r in range(4):
-                nc.tensor.matmul(out=tb[:, r * P:(r + 1) * P],
-                                 lhsT=ident_b[:, 20 + r:21 + r].to_broadcast([P, P]),
-                                 rhs=b2d[:], start=True, stop=True)
-            nc.scalar.copy(out=bv_bc[:], in_=tb[:])
+            nc.sync.dma_start(out=bv_bc[:], in_=qkv_bias[5 * GW:6 * GW].partition_broadcast(P))
 
         def x_turn(i):
             words = x_sbs[i // 2][:, i % 2, :].bitcast(F32)
@@ -218,20 +213,20 @@ def tile_attentioncore_pa_kernel(tc, x, qkv_kernel, qkv_bias, cos_table, sin_tab
                                  is_transpose=True, start=False, stop=True)
 
         def leave(m):
-            key = m // 4 if m < 16 else 4 + (m - 16) // 2
-            width = GW if m < 16 else 2 * P
+            key = m // 4 if m < 16 else (4, 4, 5, 6)[m - 16]
+            width = GW if m < 16 else (2 * P if m < 18 else P)
             if key not in outs:
                 o_new = outp.tile([P, 4, width], F32, name="o%d" % key, tag="o", align_bytes=64)
                 outs[key] = o_new
-            col = (m % 4) * P if m < 16 else (m % 2) * P
+            col = (m % 4) * P if m < 16 else ((m % 2) * P if m < 18 else 0)
             nc.scalar.copy(out=outs[key][:, :, col:col + P],
                            in_=bks[m][:, 0, :].rearrange("p (i c) -> p i c", i=4))
 
         def store_q(n):
             nc.sync.dma_start(out=q3[:, :, n * GW:(n + 1) * GW], in_=outs[n][:])
 
-        def store_k(h):
-            nc.scalar.dma_start(out=k3[:, :, h * 2 * P:(h + 1) * 2 * P], in_=outs[4 + h][:])
+        def store_k(key, c0, c1):
+            nc.sync.dma_start(out=k3[:, :, c0:c1], in_=outs[key][:])
 
         def v_out(i):
             vo = vop.tile([P, GW], F32, name="vo%d" % i, tag="vo")
@@ -265,6 +260,7 @@ def tile_attentioncore_pa_kernel(tc, x, qkv_kernel, qkv_bias, cos_table, sin_tab
         for n in range(2, NGRP):
             for g in range(NG):
                 load_w(n, g)
+        vbias()
         make_identity(nc, ident_f[:])
         consts_v()
         copy(0, 0, "V", "S", 0, 512)
@@ -356,8 +352,6 @@ def tile_attentioncore_pa_kernel(tc, x, qkv_kernel, qkv_bias, cos_table, sin_tab
                     back(m)
                     leave(m)
                 store_q(n - 1)
-                if n == 4:
-                    vbias()
                 for g in (0, 1, 2, 3):
                     quant(n + 1, g)
             else:
@@ -366,11 +360,13 @@ def tile_attentioncore_pa_kernel(tc, x, qkv_kernel, qkv_bias, cos_table, sin_tab
                     if i < 2:
                         v_out_sg(i)
                         v_store(i)
-                for m in range(16, 20):
-                    back(m)
-                    leave(m)
-                    if m % 2 == 1:
-                        store_k((m - 16) // 2)
                 for i in range(2, 4):
                     v_out(i)
                     v_store(i)
+                for m in range(16, 20):
+                    back(m)
+                    leave(m)
+                    if m == 17:
+                        store_k(4, 0, 2 * P)
+                    if m > 17:
+                        store_k(m - 13, (m - 16) * P, (m - 15) * P)

@@ -320,6 +320,10 @@ def tile_attentioncore_pa_kernel(tc, x, qkv_kernel, qkv_bias, cos_table, sin_tab
         quant(1, 0)
         for m in range(4, 8):
             mx(m, 0)
+        rot(0)
+        rot(1)
+        back(0)
+        back(1)
         copy(1, 2, "V", "S", 0, 224)
         copy(1, 2, "S", "S", 224, GW)
         quant(1, 1)
@@ -333,40 +337,37 @@ def tile_attentioncore_pa_kernel(tc, x, qkv_kernel, qkv_bias, cos_table, sin_tab
         quant(1, 3)
         for m in range(4, 8):
             mx(m, 3)
+        leave(0)
+        leave(1)
 
-        for n in range(1, NGRP):
-            for m in range(4 * n - 4, 4 * n):
+        for k in range(4):
+            batch = range(4 * k + 2, 4 * k + 6 if k < 3 else 20)
+            if k > 0:
+                for g in range(NG):
+                    for m in range(4 * k + 4, 4 * k + 8):
+                        mx(m, g)
+            for m in batch:
                 rot(m)
-            if n + 1 < NGRP:
-                copy(n + 1, 1, "G", (1, 3))
-                copy(n + 1, 3, "G", (1, 3), 0, 320)
-                copy(n + 1, 0, "S")
-                copy(n + 1, 2, "S")
-                copy(n + 1, 3, "S", (1, 3), 320, GW)
-            if n < 5:
-                if n > 1 or False:
-                    for g in range(NG):
-                        for m in range(4 * n, 4 * n + 4):
-                            mx(m, g)
-                for m in range(4 * n - 4, 4 * n):
-                    back(m)
-                    leave(m)
-                store_q(n - 1)
-                for g in (0, 1, 2, 3):
-                    quant(n + 1, g)
+            copy(k + 2, 1, "G", (1, 3))
+            copy(k + 2, 3, "G", (1, 3), 0, 320)
+            copy(k + 2, 0, "S")
+            copy(k + 2, 2, "S")
+            copy(k + 2, 3, "S", (1, 3), 320, GW)
+            for m in batch:
+                back(m)
+                leave(m)
+                if m == 4 * k + 3:
+                    store_q(k)
+                if m == 17:
+                    store_k(4, 0, 2 * P)
+                if m > 17:
+                    store_k(m - 13, (m - 16) * P, (m - 15) * P)
+            for g in range(NG):
+                quant(k + 2, g)
+        for i in range(4):
+            mx_tile(20 + i)
+            if i < 2:
+                v_out_sg(i)
             else:
-                for i in range(4):
-                    mx_tile(20 + i)
-                    if i < 2:
-                        v_out_sg(i)
-                        v_store(i)
-                for i in range(2, 4):
-                    v_out(i)
-                    v_store(i)
-                for m in range(16, 20):
-                    back(m)
-                    leave(m)
-                    if m == 17:
-                        store_k(4, 0, 2 * P)
-                    if m > 17:
-                        store_k(m - 13, (m - 16) * P, (m - 15) * P)
+                v_out(i)
+            v_store(i)

@@ -322,8 +322,6 @@ def tile_attentioncore_pa_kernel(tc, x, qkv_kernel, qkv_bias, cos_table, sin_tab
             mx(m, 0)
         rot(0)
         rot(1)
-        back(0)
-        back(1)
         copy(1, 2, "V", "S", 0, 224)
         copy(1, 2, "S", "S", 224, GW)
         quant(1, 1)
@@ -337,8 +335,6 @@ def tile_attentioncore_pa_kernel(tc, x, qkv_kernel, qkv_bias, cos_table, sin_tab
         quant(1, 3)
         for m in range(4, 8):
             mx(m, 3)
-        leave(0)
-        leave(1)
 
         for k in range(4):
             batch = range(4 * k + 2, 4 * k + 6 if k < 3 else 20)
@@ -353,7 +349,7 @@ def tile_attentioncore_pa_kernel(tc, x, qkv_kernel, qkv_bias, cos_table, sin_tab
             copy(k + 2, 0, "S")
             copy(k + 2, 2, "S")
             copy(k + 2, 3, "S", (1, 3), 320, GW)
-            for m in batch:
+            for m in (range(0, 6) if k == 0 else batch):
                 back(m)
                 leave(m)
                 if m == 4 * k + 3:

@@ -360,10 +360,13 @@ def tile_attentioncore_pa_kernel(tc, x, qkv_kernel, qkv_bias, cos_table, sin_tab
                     store_k(m - 13, (m - 16) * P, (m - 15) * P)
             for g in range(NG):
                 quant(k + 2, g)
-        for i in range(4):
+        for i in range(3):
             mx_tile(20 + i)
-            if i < 2:
-                v_out_sg(i)
-            else:
-                v_out(i)
+            v_out(i)
             v_store(i)
+        mx_tile(23)
+        vo3 = vop.tile([P, GW], F32, name="vo3", tag="vo")
+        for c in range(2):
+            half = slice(c * 256, (c + 1) * 256)
+            nc.vector.tensor_tensor(out=vo3[:, half], in0=bks[23][:, 0, half], in1=bv_bc[:, half], op=ADD)
+            (nc.sync, nc.scalar)[c].dma_start(out=v2[3 * P:4 * P, half], in_=vo3[:, half])

from contextlib import ExitStack

import concourse.mybir as mybir
from concourse.masks import make_identity

S_TOK, H, QKV = 512, 2048, 3072
FLOPS = 2 * S_TOK * H * QKV

F32 = mybir.dt.float32
BF16 = mybir.dt.bfloat16
U32 = mybir.dt.uint32
U8 = mybir.dt.uint8
E5X4 = mybir.dt.float8_e5m2_x4
ADD = mybir.AluOpType.add
MULT = mybir.AluOpType.mult

P = 128
NG = 4
NGRP = 6
GW = 512


def tile_attentioncore_pa_kernel(tc, x, qkv_kernel, qkv_bias, cos_table, sin_table,
                                             out_0, out_1, out_2):
    nc = tc.nc
    with ExitStack() as ctx:
        const = ctx.enter_context(tc.tile_pool(name="const", bufs=1))
        rawp = ctx.enter_context(tc.tile_pool(name="rawp", bufs=4))
        grps = ctx.enter_context(tc.tile_pool(name="grps", bufs=4))
        grpv = ctx.enter_context(tc.tile_pool(name="grpv", bufs=1))
        grpg = ctx.enter_context(tc.tile_pool(name="grpg", bufs=1))
        vop = ctx.enter_context(tc.tile_pool(name="vop", bufs=4))
        codes = ctx.enter_context(tc.tile_pool(name="codes", bufs=1))
        tup = ctx.enter_context(tc.tile_pool(name="tup", bufs=4))
        outp = ctx.enter_context(tc.tile_pool(name="outp", bufs=4))
        bank = ctx.enter_context(tc.psum_pool(name="bank", bufs=8))
        ctx.enter_context(tc.manual_schedule())

        b2d = const.tile([P, P], BF16, name="b2d", tag="b2d")
        xs_a = outp.tile([P, 2, H], BF16, name="xs_a", tag="o", align_bytes=64)
        xs_b = outp.tile([P, 2, H], BF16, name="xs_b", tag="o", align_bytes=64)
        x_sbs = (xs_a, xs_b)
        ident_f = const.tile([P, P], F32, name="ident_f", tag="ident_f")
        ident_b = const.tile([P, P], BF16, name="ident_b", tag="ident_b")
        perm_f = const.tile([P, P], F32, name="perm_f", tag="perm_f")
        e_c = const.tile([P, 4, P], BF16, name="e_c", tag="e_c")
        e_s = const.tile([P, 4, P], BF16, name="e_s", tag="e_s")
        cs = const.tile([P, 2, S_TOK], BF16, name="cs", tag="cs")
        b_pp = const.tile([P, P], F32, name="b_pp", tag="b_pp")
        bv_bc = const.tile([P, GW], BF16, name="bv_bc", tag="bv_bc")
        xc = codes.tile([P, NG, S_TOK], U32, name="xc", tag="xc", align_bytes=64)
        xs = codes.tile([P, NG, S_TOK], U8, name="xs", tag="xs", align_bytes=64)
        wcs = []
        wss = []
        for n in range(NGRP):
            wc = codes.tile([P, NG, GW], U32, name="wc%d" % n, tag="wc%d" % n, align_bytes=64)
            ws = codes.tile([P, NG, GW], U8, name="ws%d" % n, tag="ws%d" % n, align_bytes=64)
            wcs.append(wc)
            wss.append(ws)
        raws = {}
        gxs = {}
        grs = {}
        bks = {}
        tus = {}
        outs = {}
        vos = {}
        q3 = out_0.rearrange("s h d -> s (h d)").rearrange("(i p) c -> p i c", p=P)
        k3 = out_1.rearrange("s h d -> s (h d)").rearrange("(i p) c -> p i c", p=P)
        v2 = out_2.rearrange("s h d -> s (h d)")

        def load_tabs():
            nc.scalar.dma_start(out=e_c[:, :, 0:32], in_=cos_table.rearrange("(i p) j -> p i j", p=P))
            nc.scalar.dma_start(out=e_s[:, :, 0:32], in_=sin_table.rearrange("(i p) j -> p i j", p=P))
            nc.scalar.dma_start(out=b2d[0:24, :], in_=qkv_bias.rearrange("(r c) -> r c", c=P))

        def load_x(i):
            nc.sync.dma_start(out=x_sbs[i // 2][:, i % 2, :], in_=x[i * P:(i + 1) * P, :])

        def load_w(n, g):
            if n not in raws:
                raw_new = rawp.tile([P, NG, 4, GW], BF16, name="raw%d" % n, tag="raw")
                raws[n] = raw_new
            nc.sync.dma_start(
                out=raws[n][:, g, :, :],
                in_=qkv_kernel[g * 512:(g + 1) * 512, n * GW:(n + 1) * GW].rearrange(
                    "(p j) w -> p j w", j=4))

        def consts_v():
            nc.vector.tensor_copy(out=ident_b[:], in_=ident_f[:])
            pv = perm_f[:].rearrange("p (a h j) -> p a h j", a=2, h=2)
            iv = ident_f[:].rearrange("p (a h j) -> p a h j", a=2, h=2)
            nc.vector.tensor_copy(out=pv[:, :, 0, :], in_=iv[:, :, 1, :])
            nc.vector.tensor_copy(out=pv[:, :, 1, :], in_=iv[:, :, 0, :])

        def tables_v():
            nc.vector.tensor_copy(out=e_c[:, :, 32:64], in_=e_c[:, :, 0:32])
            nc.vector.tensor_scalar_mul(out=e_s[:, :, 32:64], in0=e_s[:, :, 0:32], scalar1=-1.0)
            nc.vector.tensor_copy(out=e_c[:, :, 64:128], in_=e_c[:, :, 0:64])
            nc.vector.tensor_copy(out=e_s[:, :, 64:128], in_=e_s[:, :, 0:64])

        def new_bank(key, shape, dtype):
            bk = bank.tile(shape, dtype, name="bk_%s" % key, tag="bk")
            bks[key] = bk
            return bk

        def table_pe():
            tb = new_bank("tb0", [P, 2, S_TOK], BF16)
            for i in range(2):
                for b in range(4):
                    nc.tensor.transpose(tb[:, i, b * P:(b + 1) * P], (e_c, e_s)[i][:, b, :], ident_b[:])
            tb = new_bank("tb1", [P, P], BF16)
            nc.tensor.transpose(tb[:], b2d[:], ident_b[:])

        def table_out():
            nc.scalar.copy(out=cs[:], in_=bks["tb0"][:])
            nc.scalar.copy(out=b_pp[:], in_=bks["tb1"][:])

        def vbias():
            nc.sync.dma_start(out=bv_bc[:], in_=qkv_bias[5 * GW:6 * GW].partition_broadcast(P))

        def x_turn(i):
            words = x_sbs[i // 2][:, i % 2, :].bitcast(F32)
            for gp in range(2):
                xt = new_bank("xt%d%d" % (i, gp), [P, 2, 2, P], F32)
                for a in range(2):
                    g = 2 * gp + a
                    for u in range(2):
                        nc.tensor.transpose(xt[:, a, u, :], words[:, 256 * g + u:256 * (g + 1):2], ident_f[:])

        def x_out(i, gp, eng):
            if i // 2 not in gxs:
                gx = outp.tile([P, 2, NG, GW], BF16, name="gx%d" % (i // 2), tag="o", align_bytes=64)
                gxs[i // 2] = gx
            dst = gxs[i // 2][:, i % 2, 2 * gp:2 * gp + 2, :].bitcast(F32).rearrange("p g (r u) -> p g r u", u=2)
            src = bks["xt%d%d" % (i, gp)][:].rearrange("p g u r -> p g r u")
            if eng == "V":
                nc.vector.tensor_copy(out=dst, in_=src)
            else:
                nc.scalar.copy(out=dst, in_=src)

        def quant_x(g, i):
            nc.vector.quantize_mx(out=xc[:, g, i * P:(i + 1) * P].bitcast(E5X4), scales=xs[:, g, i * P:(i + 1) * P],
                                  in_=gxs[i // 2][:, i % 2, g, :])

        def unit_tile(n, g, pool):
            if (n, g) not in grs:
                if pool == "S":
                    gr = grps.tile([P, 4 * GW], BF16, name="gr%d%d" % (n, g), tag="grs", align_bytes=64)
                    grs[(n, g)] = gr[:]
                elif pool == "V":
                    gr = grpv.tile([P, 4 * GW], BF16, name="gr%d%d" % (n, g), tag="grv", align_bytes=64)
                    grs[(n, g)] = gr[:]
                else:
                    gr = grpg.tile([P, 2, 4 * GW], BF16, name="grg%d" % n, tag="grg", align_bytes=64)
                    grs[(n, pool[0])] = gr[:, 0, :]
                    grs[(n, pool[1])] = gr[:, 1, :]
            return grs[(n, g)]

        def copy(n, g, eng, pool=None, c0=0, c1=GW):
            gr = unit_tile(n, g, pool or eng)[:, 4 * c0:4 * c1]
            raw = raws[n][:, g, :, c0:c1]
            if eng != "G":
                dst = gr.rearrange("p (c i j) -> p c j i", i=4, j=4)
                src = raw.rearrange("p j (c i) -> p c j i", i=4)
            else:
                dst = gr.rearrange("p (w j) -> p w j", j=4)
                src = raw.rearrange("p j w -> p w j")
            if eng == "V":
                nc.vector.tensor_copy(out=dst, in_=src)
            elif eng == "S":
                nc.scalar.copy(out=dst, in_=src)
            else:
                nc.gpsimd.tensor_scalar(out=dst, in0=src, scalar1=1.0, scalar2=0.0, op0=MULT, op1=ADD)

        def quant(n, g):
            nc.vector.quantize_mx(out=wcs[n][:, g, :].bitcast(E5X4), scales=wss[n][:, g, :],
                                  in_=grs[(n, g)])

        def mx(m, g):
            if g == 0:
                new_bank(m, [P, 1, S_TOK], F32)
            acc = bks[m][:, 0, :]
            if m < 20:
                n = m // 4
                cols = slice((m % 4) * P, (m % 4 + 1) * P)
                nc.tensor.matmul_mx(out=acc,
                                    lhsT=wcs[n][:, g, cols].bitcast(E5X4), lhsT_scale=wss[n][:, g, cols],
                                    rhs=xc[:, g, :].bitcast(E5X4), rhs_scale=xs[:, g, :],
                                    start=(g == 0), stop=(g == NG - 1))
            else:
                cols = slice((m - 20) * P, (m - 19) * P)
                nc.tensor.matmul_mx(out=acc,
                                    lhsT=xc[:, g, cols].bitcast(E5X4), lhsT_scale=xs[:, g, cols],
                                    rhs=wcs[5][:, g, :].bitcast(E5X4), rhs_scale=wss[5][:, g, :],
                                    start=(g == 0), stop=(g == NG - 1))

        def mx_tile(m):
            for g in range(NG):
                mx(m, g)

        def rot(m):
            tu = tup.tile([P, 2, S_TOK], F32, name="tu%d" % m, tag="tu")
            tus[m] = tu
            nc.vector.scalar_tensor_tensor(out=tu[:], in0=bks[m][:].to_broadcast([P, 2, S_TOK]),
                                           scalar=b_pp[:, m:m + 1], in1=cs[:], op0=ADD, op1=MULT)

        def back(m):
            tr = bks[m][:, 0, :].rearrange("p (i c) -> p i c", i=4)
            for i in range(4):
                nc.tensor.matmul(out=tr[:, i, :], lhsT=tus[m][:, 0, i * P:(i + 1) * P], rhs=ident_f[:],
                                 is_transpose=True, start=True, stop=False)
                nc.tensor.matmul(out=tr[:, i, :], lhsT=tus[m][:, 1, i * P:(i + 1) * P], rhs=perm_f[:],
                                 is_transpose=True, start=False, stop=True)

        def leave(m):
            key = m // 4 if m < 16 else (4, 4, 5, 6)[m - 16]
            width = GW if m < 16 else (2 * P if m < 18 else P)
            if key not in outs:
                o_new = outp.tile([P, 4, width], F32, name="o%d" % key, tag="o", align_bytes=64)
                outs[key] = o_new
            col = (m % 4) * P if m < 16 else ((m % 2) * P if m < 18 else 0)
            nc.scalar.copy(out=outs[key][:, :, col:col + P],
                           in_=bks[m][:, 0, :].rearrange("p (i c) -> p i c", i=4))

        def store_q(n):
            nc.sync.dma_start(out=q3[:, :, n * GW:(n + 1) * GW], in_=outs[n][:])

        def store_k(key, c0, c1):
            nc.sync.dma_start(out=k3[:, :, c0:c1], in_=outs[key][:])

        def v_out(i):
            vo = vop.tile([P, GW], F32, name="vo%d" % i, tag="vo")
            vos[i] = vo
            nc.vector.tensor_tensor(out=vo[:], in0=bks[20 + i][:, 0, :], in1=bv_bc[:], op=ADD)

        def v_out_sg(i):
            va = vop.tile([P, GW], F32, name="va%d" % i, tag="va")
            vo = vop.tile([P, GW], F32, name="vo%d" % i, tag="vo")
            vos[i] = vo
            nc.scalar.copy(out=va[:], in_=bks[20 + i][:, 0, :])
            nc.gpsimd.tensor_tensor(out=vo[:], in0=va[:], in1=bv_bc[:], op=ADD)

        def v_store(i):
            nc.sync.dma_start(out=v2[i * P:(i + 1) * P, :], in_=vos[i][:])

        nc.gpsimd.memset(b2d[:], 0.0)
        load_tabs()
        load_w(0, 0)
        load_x(0)
        load_x(1)
        load_x(2)
        load_x(3)
        load_w(0, 1)
        load_w(0, 2)
        load_w(0, 3)
        load_w(1, 0)
        load_w(1, 1)
        load_w(1, 2)
        load_w(1, 3)
        for n in range(2, NGRP):
            for g in range(NG):
                load_w(n, g)
        vbias()
        make_identity(nc, ident_f[:])
        consts_v()
        copy(0, 0, "V", "S", 0, 512)
        tables_v()
        quant(0, 0)
        x_turn(0)
        x_out(0, 0, "S")
        x_out(0, 1, "S")
        quant_x(0, 0)
        quant_x(1, 0)
        quant_x(2, 0)
        quant_x(3, 0)
        x_turn(1)
        x_out(1, 0, "S")
        x_out(1, 1, "S")
        quant_x(0, 1)
        quant_x(1, 1)
        quant_x(2, 1)
        quant_x(3, 1)
        x_turn(2)
        x_out(2, 0, "S")
        x_out(2, 1, "S")
        quant_x(0, 2)
        quant_x(1, 2)
        quant_x(2, 2)
        quant_x(3, 2)
        x_turn(3)
        table_pe()
        x_out(3, 0, "S")
        x_out(3, 1, "V")
        quant_x(0, 3)
        for m in range(0, 4):
            mx(m, 0)
        quant_x(1, 3)
        quant_x(2, 3)
        quant_x(3, 3)
        copy(0, 1, "V", "S", 0, 256)
        copy(0, 1, "S", "S", 256, GW)
        table_out()
        copy(0, 2, "V", "S", 0, 256)
        copy(0, 2, "S", "S", 256, GW)
        quant(0, 1)
        for m in range(0, 4):
            mx(m, 1)
        copy(0, 3, "V", "S", 0, 256)
        copy(0, 3, "S", "S", 256, GW)
        quant(0, 2)
        for m in range(0, 4):
            mx(m, 2)
        copy(1, 0, "V", "S", 0, 224)
        copy(1, 0, "S", "S", 224, GW)
        quant(0, 3)
        for m in range(0, 4):
            mx(m, 3)
        copy(1, 1, "V", (1, 3), 0, 224)
        copy(1, 1, "S", (1, 3), 224, GW)
        quant(1, 0)
        for m in range(4, 8):
            mx(m, 0)
        rot(0)
        rot(1)
        copy(1, 2, "V", "S", 0, 224)
        copy(1, 2, "S", "S", 224, GW)
        quant(1, 1)
        for m in range(4, 8):
            mx(m, 1)
        copy(1, 3, "V", (1, 3), 0, 224)
        copy(1, 3, "S", (1, 3), 224, GW)
        quant(1, 2)
        for m in range(4, 8):
            mx(m, 2)
        quant(1, 3)
        for m in range(4, 8):
            mx(m, 3)

        for k in range(4):
            batch = range(4 * k + 2, 4 * k + 6 if k < 3 else 20)
            if k > 0:
                for g in range(NG):
                    for m in range(4 * k + 4, 4 * k + 8):
                        mx(m, g)
            for m in batch:
                rot(m)
            copy(k + 2, 1, "G", (1, 3))
            copy(k + 2, 3, "G", (1, 3), 0, 320)
            copy(k + 2, 0, "S")
            copy(k + 2, 2, "S")
            copy(k + 2, 3, "S", (1, 3), 320, GW)
            for m in (range(0, 6) if k == 0 else batch):
                back(m)
                leave(m)
                if m == 4 * k + 3:
                    store_q(k)
                if m == 17:
                    store_k(4, 0, 2 * P)
                if m > 17:
                    store_k(m - 13, (m - 16) * P, (m - 15) * P)
            for g in range(NG):
                quant(k + 2, g)
        for i in range(3):
            mx_tile(20 + i)
            v_out(i)
            v_store(i)
        mx_tile(23)
        vo3 = vop.tile([P, GW], F32, name="vo3", tag="vo")
        for c in range(2):
            half = slice(c * 256, (c + 1) * 256)
            nc.vector.tensor_tensor(out=vo3[:, half], in0=bks[23][:, 0, half], in1=bv_bc[:, half], op=ADD)
            (nc.sync, nc.scalar)[c].dma_start(out=v2[3 * P:4 * P, half], in_=vo3[:, half])
